import numpy as np
import ml_dtypes


def mxq(x, axis, fmt="e4m3"):
    dtype, down = {"e4m3": (ml_dtypes.float8_e4m3fn, 7), "e5m2": (ml_dtypes.float8_e5m2, 14)}[fmt]
    v = np.moveaxis(np.asarray(x, np.float32).astype(ml_dtypes.bfloat16).astype(np.float64), axis, -1)
    blocks = v.reshape(v.shape[:-1] + (-1, 32))
    amax = np.abs(blocks).max(-1, keepdims=True)
    byte = np.maximum(np.where(amax > 0, np.frexp(amax)[1] - 1 + 127, 0) - down, 1)
    scale = np.exp2(byte - 127.0)
    codes = (blocks / scale).astype(np.float32).astype(dtype).astype(np.float64)
    return np.moveaxis((codes * scale).reshape(v.shape), -1, axis)


WIDE = False


def mx_kscale(k):
    if not WIDE:
        return np.ones(k)
    levels = np.array([10, -10, 5, -5, 0])
    a = np.random.permutation(np.resize(levels, k // 512 * 4)).reshape(k // 512, 4)
    idx = np.arange(k)
    return np.exp2(a[idx // 512, idx % 128 // 32])


BF16 = ml_dtypes.bfloat16


def bf(x):
    return np.asarray(x, np.float32).astype(BF16)


def f64(x):
    return np.asarray(x).astype(np.float64)


B, N, D = 512, 4096, 1024
P_DROP = 0.25
P_ZERO = 0.125
LN_EPS = 1e-5


def setup_inputs():
    s = mx_kscale(N)
    x = np.random.standard_normal((B, N)) * (np.random.uniform(size=(B, N)) >= P_ZERO) * s
    drop_mask = (np.random.uniform(size=(B, N)) >= P_DROP).astype(np.float64)
    return {"x": bf(x), "drop_mask": bf(drop_mask),
            "W": bf(np.random.standard_normal((D, N)) * 0.8 / np.sqrt(N) / s[None, :]),
            "b1": bf(np.random.standard_normal(D) * 0.1), "b2": bf(np.random.standard_normal(N) * 0.1 / s),
            "gamma": bf(1.0 + 0.1 * np.random.standard_normal(D)), "beta": bf(0.1 * np.random.standard_normal(D))}


def reference(x, drop_mask, W, b1, b2, gamma, beta):
    x, W = f64(x), f64(W)
    h = x * f64(drop_mask) / (1.0 - P_DROP)
    enc = np.tanh((mxq(h, 1, "e4m3") @ mxq(W, 1, "e4m3").T) + f64(b1))
    recon = (mxq(enc, 1, "e4m3") @ mxq(W, 0, "e4m3")) + f64(b2)
    mu = np.mean(enc, axis=-1, keepdims=True)
    var = np.mean((enc - mu) ** 2, axis=-1, keepdims=True)
    final = (enc - mu) / np.sqrt(var + LN_EPS) * f64(gamma) + f64(beta)
    nz = (x != 0).astype(np.float64)
    per = np.sum((nz * (x - recon)) ** 2, axis=-1) / np.sum(nz, axis=-1)
    recon_loss = np.sum(per).reshape(1)
    return final, recon_loss

@@ -1,0 +1,260 @@
+from contextlib import ExitStack
+
+import concourse.mybir as mybir
+from concourse.masks import make_identity
+
+B, N, D = 512, 4096, 1024
+FLOPS = 2 * 2 * B * N * D
+KEEP_SCALE = 1.0 / 0.75
+LN_EPS = 1e-5
+
+P = 128
+K_PASS = 512
+N_TILE = 512
+B_TILES = B // P
+D_TILES = D // P
+N_PASSES = N // K_PASS
+D_PASSES = D // K_PASS
+CHUNK = 1024
+CHUNKS = N // CHUNK
+VECTOR_COLS = 352
+
+BF16 = mybir.dt.bfloat16
+F32 = mybir.dt.float32
+U32 = mybir.dt.uint32
+U8 = mybir.dt.uint8
+FP8X4 = mybir.dt.float8_e4m3fn_x4
+ALU = mybir.AluOpType
+ACT = mybir.ActivationFunctionType
+AXIS_X = mybir.AxisListType.X
+
+
+def tile_multipleembedding_kernel(tc, x, drop_mask, W, b1, b2, gamma, beta, out_0, out_1):
+    nc = tc.nc
+    with ExitStack() as ctx:
+        const = ctx.enter_context(tc.tile_pool(name="const", bufs=1))
+        keep = ctx.enter_context(tc.tile_pool(name="keep", bufs=1))
+        psum_t = ctx.enter_context(tc.psum_pool(name="psum_t", bufs=3))
+        psum_1 = ctx.enter_context(tc.psum_pool(name="psum_1", bufs=2))
+        psum_2 = ctx.enter_context(tc.psum_pool(name="psum_2", bufs=3))
+
+        ident_f = const.tile([P, P], F32, name="ident_f")
+        make_identity(nc, ident_f[:])
+        ident_b = const.tile([P, P], BF16, name="ident_b")
+        make_identity(nc, ident_b[:])
+        spread = const.tile([P, P], F32, name="spread")
+        nc.vector.memset(spread[:], 0.0)
+        neg_half = const.tile([P, 1], F32, name="neg_half")
+        nc.vector.memset(neg_half[:], -0.5)
+        b1_b = const.tile([P, D], BF16, name="b1_b")
+        nc.scalar.dma_start(out=b1_b[:], in_=b1.partition_broadcast(P))
+        b2_b = const.tile([P, N], BF16, name="b2_b")
+        nc.scalar.dma_start(out=b2_b[:], in_=b2.partition_broadcast(P))
+        gamma_b = const.tile([P, D], BF16, name="gamma_b")
+        nc.scalar.dma_start(out=gamma_b[:], in_=gamma.partition_broadcast(P))
+        beta_b = const.tile([P, D], BF16, name="beta_b")
+        nc.scalar.dma_start(out=beta_b[:], in_=beta.partition_broadcast(P))
+
+        wt_codes = keep.tile([P, N_PASSES, D], U32, name="wt_codes", align_bytes=64)
+        wt_scales = keep.tile([P, N_PASSES, D], U8, name="wt_scales", align_bytes=64)
+        w2_codes = keep.tile([P, D_PASSES, N], U32, name="w2_codes", align_bytes=64)
+        w2_scales = keep.tile([P, D_PASSES, N], U8, name="w2_scales", align_bytes=64)
+        x_sb = [keep.tile([P, N], BF16, name="x_sb%d" % bt) for bt in range(B_TILES)]
+        h_codes = [keep.tile([P, N_PASSES * P], U32, name="h_codes%d" % bt, align_bytes=64) for bt in range(B_TILES)]
+        h_scales = [keep.tile([P, N_PASSES * P], U8, name="h_scales%d" % bt, align_bytes=64) for bt in range(B_TILES)]
+        count = keep.tile([P, B_TILES], F32, name="count")
+        row_loss = keep.tile([P, B_TILES], F32, name="row_loss")
+
+        w_view = W.rearrange("(t p) n -> p t n", p=P)
+
+        with tc.tile_pool(name="wstage", bufs=2) as stage:
+            w_nat = {}
+            xm_tiles = {}
+
+            def load(c):
+                w_nat[c] = stage.tile([P, D_TILES, CHUNK], BF16, name="w_nat", tag="w_nat")
+                nc.sync.dma_start(out=w_nat[c][:], in_=w_view[:, :, c * CHUNK : (c + 1) * CHUNK])
+                nc.sync.dma_start(out=x_sb[c][:], in_=x[c * P : (c + 1) * P, :])
+                xm_tiles[c] = stage.tile([P, N], BF16, name="mask", tag="mask")
+                nc.sync.dma_start(out=xm_tiles[c][:], in_=drop_mask[c * P : (c + 1) * P, :])
+
+            def prepare_w_first(c):
+                wn = w_nat[c]
+                for gl in range(CHUNK // K_PASS):
+                    g = c * (CHUNK // K_PASS) + gl
+                    for half in range(2):
+                        grouped = stage.tile([P, 4 * N_TILE], BF16, name="wtg", tag="wtg", bufs=3, align_bytes=64)
+                        g_words = grouped[:].bitcast(F32).rearrange("p (c u) -> p c u", u=2)
+                        for j in range(2):
+                            bank = psum_t.tile([P, N_TILE], F32, name="bank", tag="tp")
+                            planes = bank[:].rearrange("p (u c) -> p u c", u=2)
+                            for dd in range(2):
+                                d_tile = 4 * half + 2 * j + dd
+                                words = wn[:, d_tile, :].bitcast(F32)
+                                for u in range(2):
+                                    first = 256 * gl + P * u
+                                    nc.tensor.transpose(
+                                        planes[:, u, P * dd : P * (dd + 1)], words[:, first : first + P], ident_f[:]
+                                    )
+                            nc.scalar.copy(
+                                out=g_words[:, 256 * j : 256 * (j + 1), :],
+                                in_=bank[:].rearrange("p (u c) -> p c u", u=2),
+                            )
+                        cols = slice(N_TILE * half, N_TILE * (half + 1))
+                        nc.vector.quantize_mx(
+                            out=wt_codes[:, g, cols].bitcast(FP8X4), scales=wt_scales[:, g, cols], in_=grouped[:]
+                        )
+
+            def prepare_w_second(c):
+                wn = w_nat[c]
+                for gd in range(D_PASSES):
+                    for blk in range(CHUNK // N_TILE):
+                        grouped = stage.tile([P, N_TILE, 4], BF16, name="w2g", tag="w2g", bufs=3, align_bytes=64)
+                        first = N_TILE * blk
+                        for engine_copy, lo, hi in (
+                            (nc.vector.tensor_copy, 0, VECTOR_COLS),
+                            (nc.scalar.copy, VECTOR_COLS, N_TILE),
+                        ):
+                            engine_copy(
+                                out=grouped[:, lo:hi, :].rearrange("p (c i) t -> p c t i", i=4),
+                                in_=wn[:, 4 * gd : 4 * gd + 4, first + lo : first + hi].rearrange(
+                                    "p t (c i) -> p c t i", i=4
+                                ),
+                            )
+                        cols = slice(c * CHUNK + first, c * CHUNK + first + N_TILE)
+                        nc.vector.quantize_mx(
+                            out=w2_codes[:, gd, cols].bitcast(FP8X4),
+                            scales=w2_scales[:, gd, cols],
+                            in_=grouped[:].rearrange("p c t -> p (c t)"),
+                        )
+
+            def prepare_h(bt):
+                xm = xm_tiles[bt]
+                nc.vector.tensor_tensor(out=xm[:], in0=x_sb[bt][:], in1=xm[:], op=ALU.mult)
+                words = xm[:].bitcast(F32)
+                grouped = stage.tile([P, 4 * N_PASSES * P], BF16, name="hg", tag="hg", bufs=1, align_bytes=64)
+                g_view = grouped[:].rearrange("p (c u e) -> p c u e", u=2, e=2)
+                for j in range(N_PASSES // 2):
+                    bank = psum_t.tile([P, N_TILE], F32, name="bank", tag="tp")
+                    planes = bank[:].rearrange("p (u c) -> p u c", u=2)
+                    for gl in range(2):
+                        for u in range(2):
+                            first = 256 * (2 * j + gl) + P * u
+                            nc.tensor.transpose(
+                                planes[:, u, P * gl : P * (gl + 1)], words[:, first : first + P], ident_f[:]
+                            )
+                    nc.scalar.activation(
+                        out=g_view[:, 256 * j : 256 * (j + 1), :, :],
+                        in_=bank[:].bitcast(BF16).rearrange("p (u c e) -> p c u e", u=2, e=2),
+                        func=ACT.Copy,
+                        scale=KEEP_SCALE,
+                    )
+                nc.vector.quantize_mx(out=h_codes[bt][:].bitcast(FP8X4), scales=h_scales[bt][:], in_=grouped[:])
+
+            load(0)
+            load(1)
+            for c in range(CHUNKS):
+                prepare_w_first(c)
+                prepare_w_second(c)
+                prepare_h(c)
+                if c + 2 < CHUNKS:
+                    load(c + 2)
+
+        with tc.tile_pool(name="post", bufs=2) as post, tc.tile_pool(name="small", bufs=2) as small:
+            for bt in range(B_TILES):
+                rows = slice(bt * P, (bt + 1) * P)
+                xt = x_sb[bt]
+
+                nz = post.tile([P, N], BF16, name="nz", tag="nz", bufs=1)
+                nc.vector.tensor_single_scalar(out=nz[:], in_=xt[:], scalar=0.0, op=ALU.not_equal)
+                nc.scalar.activation(out=nz[:], in_=nz[:], func=ACT.Copy, accum_out=count[:, bt : bt + 1])
+
+                pre = post.tile([P, D], F32, name="pre", tag="pre")
+                for half in range(D // N_TILE):
+                    cols = slice(N_TILE * half, N_TILE * (half + 1))
+                    acc = psum_1.tile([P, N_TILE], F32, name="acc1", tag="acc1")
+                    for g in range(N_PASSES):
+                        m_cols = slice(P * g, P * (g + 1))
+                        nc.tensor.matmul_mx(
+                            out=acc[:],
+                            lhsT=h_codes[bt][:, m_cols].bitcast(FP8X4),
+                            lhsT_scale=h_scales[bt][:, m_cols],
+                            rhs=wt_codes[:, g, cols].bitcast(FP8X4),
+                            rhs_scale=wt_scales[:, g, cols],
+                            start=(g == 0),
+                            stop=(g == N_PASSES - 1),
+                        )
+                    nc.vector.tensor_tensor(out=pre[:, cols], in0=acc[:], in1=b1_b[:, cols], op=ALU.add)
+                enc = post.tile([P, D], F32, name="enc", tag="enc")
+                enc_sum = small.tile([P, 1], F32, name="enc_sum", tag="enc_sum")
+                nc.scalar.activation(out=enc[:], in_=pre[:], func=ACT.Tanh, accum_out=enc_sum[:])
+                enc_bf = post.tile([P, D], BF16, name="enc_bf", tag="enc_bf")
+                nc.scalar.activation(out=enc_bf[:], in_=pre[:], func=ACT.Tanh)
+
+                bank = psum_t.tile([P, D], BF16, name="bank_b", tag="tp")
+                for d_tile in range(D_TILES):
+                    d_cols = slice(P * d_tile, P * (d_tile + 1))
+                    nc.tensor.transpose(bank[:, d_cols], enc_bf[:, d_cols], ident_b[:])
+                grouped = post.tile([P, D], BF16, name="eg", tag="eg", align_bytes=64)
+                nc.scalar.copy(
+                    out=grouped[:].rearrange("p (g r t) -> p g r t", g=D_PASSES, t=4),
+                    in_=bank[:].rearrange("p (g t r) -> p g r t", g=D_PASSES, t=4),
+                )
+                e_codes = post.tile([P, D_PASSES * P], U32, name="e_codes", tag="e_codes", align_bytes=64)
+                e_scales = post.tile([P, D_PASSES * P], U8, name="e_scales", tag="e_scales", align_bytes=64)
+                nc.vector.quantize_mx(out=e_codes[:].bitcast(FP8X4), scales=e_scales[:], in_=grouped[:])
+
+                neg_mean = small.tile([P, 1], F32, name="neg_mean", tag="neg_mean")
+                nc.vector.tensor_scalar_mul(out=neg_mean[:], in0=enc_sum[:], scalar1=-1.0 / D)
+                sq_sum = small.tile([P, 1], F32, name="sq_sum", tag="sq_sum")
+                nc.scalar.activation(out=pre[:], in_=enc[:], func=ACT.Square, bias=neg_mean[:], accum_out=sq_sum[:])
+                var_eps = small.tile([P, 1], F32, name="var_eps", tag="var_eps")
+                nc.vector.tensor_scalar(
+                    out=var_eps[:], in0=sq_sum[:], scalar1=1.0 / D, scalar2=LN_EPS, op0=ALU.mult, op1=ALU.add
+                )
+                rstd = small.tile([P, 1], F32, name="rstd", tag="rstd")
+                nc.gpsimd.tensor_tensor(out=rstd[:], in0=var_eps[:], in1=neg_half[:], op=ALU.pow)
+                fin = post.tile([P, D], F32, name="fin", tag="fin")
+                nc.vector.scalar_tensor_tensor(
+                    out=fin[:], in0=enc[:], scalar=neg_mean[:], in1=gamma_b[:], op0=ALU.add, op1=ALU.mult
+                )
+                nc.vector.scalar_tensor_tensor(
+                    out=fin[:], in0=fin[:], scalar=rstd[:], in1=beta_b[:], op0=ALU.mult, op1=ALU.add
+                )
+                nc.sync.dma_start(out=out_0[rows, :], in_=fin[:])
+
+                tile_loss = small.tile([P, N // N_TILE], F32, name="tile_loss", tag="tile_loss")
+                for nt in range(N // N_TILE):
+                    cols = slice(N_TILE * nt, N_TILE * (nt + 1))
+                    x_less_b2 = post.tile([P, N_TILE], F32, name="xb", tag="xb", bufs=3)
+                    nc.vector.tensor_tensor(out=x_less_b2[:], in0=xt[:, cols], in1=b2_b[:, cols], op=ALU.subtract)
+                    acc = psum_2.tile([P, N_TILE], F32, name="acc2", tag="acc2")
+                    for gd in range(D_PASSES):
+                        m_cols = slice(P * gd, P * (gd + 1))
+                        nc.tensor.matmul_mx(
+                            out=acc[:],
+                            lhsT=e_codes[:, m_cols].bitcast(FP8X4),
+                            lhsT_scale=e_scales[:, m_cols],
+                            rhs=w2_codes[:, gd, cols].bitcast(FP8X4),
+                            rhs_scale=w2_scales[:, gd, cols],
+                            start=(gd == 0),
+                            stop=(gd == D_PASSES - 1),
+                        )
+                    diff = post.tile([P, N_TILE], F32, name="diff", tag="diff", bufs=3)
+                    nc.vector.tensor_tensor(out=diff[:], in0=acc[:], in1=x_less_b2[:], op=ALU.subtract)
+                    nc.vector.scalar_tensor_tensor(
+                        out=diff[:], in0=xt[:, cols], scalar=0.0, in1=diff[:], op0=ALU.not_equal, op1=ALU.mult
+                    )
+                    nc.scalar.activation(out=diff[:], in_=diff[:], func=ACT.Square, accum_out=tile_loss[:, nt : nt + 1])
+                nc.vector.tensor_reduce(out=row_loss[:, bt : bt + 1], in_=tile_loss[:], axis=AXIS_X, op=ALU.add)
+
+            inv_count = small.tile([P, B_TILES], F32, name="inv_count", tag="inv_count")
+            nc.vector.reciprocal(out=inv_count[:], in_=count[:])
+            per_row = small.tile([P, B_TILES], F32, name="per_row", tag="per_row")
+            nc.vector.tensor_tensor(out=per_row[:], in0=row_loss[:], in1=inv_count[:], op=ALU.mult)
+            nc.vector.tensor_reduce(out=spread[:, 0:1], in_=per_row[:], axis=AXIS_X, op=ALU.add)
+            bank = psum_t.tile([P, N_TILE], F32, name="bank", tag="tp")
+            nc.tensor.transpose(bank[:, 0:P], spread[:], ident_f[:])
+            total = small.tile([P, 1], F32, name="total", tag="total")
+            nc.vector.tensor_reduce(out=total[:], in_=bank[:, 0:P], axis=AXIS_X, op=ALU.add)
+            nc.sync.dma_start(out=out_1.rearrange("(a b) -> a b", a=1), in_=total[0:1, 0:1])

@@ -10,14 +10,23 @@ LN_EPS = 1e-5
 
 P = 128
 K_PASS = 512
-N_TILE = 512
+BANK_F32 = 512
+BANK_BF16 = 1024
 B_TILES = B // P
 D_TILES = D // P
+N_TILES = N // P
 N_PASSES = N // K_PASS
 D_PASSES = D // K_PASS
 CHUNK = 1024
 CHUNKS = N // CHUNK
-VECTOR_COLS = 352
+W2_CHUNK = 512
+W2_CHUNKS = N // W2_CHUNK
+RING = 4
+WINDOW_CHUNKS = 3
+V_COLS_WINDOW = 320
+V_COLS_LOOP = 0
+COUNT_BANK = 7
+LOSS_COLS = W2_CHUNKS + 1
 
 BF16 = mybir.dt.bfloat16
 F32 = mybir.dt.float32
@@ -34,9 +43,16 @@ def tile_multipleembedding_kernel(tc, x, drop_mask, W, b1, b2, gamma, beta, out_
     with ExitStack() as ctx:
         const = ctx.enter_context(tc.tile_pool(name="const", bufs=1))
         keep = ctx.enter_context(tc.tile_pool(name="keep", bufs=1))
-        psum_t = ctx.enter_context(tc.psum_pool(name="psum_t", bufs=3))
-        psum_1 = ctx.enter_context(tc.psum_pool(name="psum_1", bufs=2))
-        psum_2 = ctx.enter_context(tc.psum_pool(name="psum_2", bufs=3))
+        ring = ctx.enter_context(tc.tile_pool(name="ring", bufs=RING))
+        again = ctx.enter_context(tc.tile_pool(name="again", bufs=2))
+        psum = ctx.enter_context(tc.psum_pool(name="psum", bufs=1))
+        ctx.enter_context(tc.manual_schedule())
+
+        def bank_f32(k):
+            return psum.tile([P, BANK_F32], F32, name="bank%d" % k, tag="bank%d" % k)
+
+        def bank_bf16(k):
+            return psum.tile([P, BANK_BF16], BF16, name="bank%d" % k, tag="bank%d" % k)
 
         ident_f = const.tile([P, P], F32, name="ident_f")
         make_identity(nc, ident_f[:])
@@ -46,215 +62,440 @@ def tile_multipleembedding_kernel(tc, x, drop_mask, W, b1, b2, gamma, beta, out_
         nc.vector.memset(spread[:], 0.0)
         neg_half = const.tile([P, 1], F32, name="neg_half")
         nc.vector.memset(neg_half[:], -0.5)
-        b1_b = const.tile([P, D], BF16, name="b1_b")
-        nc.scalar.dma_start(out=b1_b[:], in_=b1.partition_broadcast(P))
-        b2_b = const.tile([P, N], BF16, name="b2_b")
-        nc.scalar.dma_start(out=b2_b[:], in_=b2.partition_broadcast(P))
+        ones_b = const.tile([P, P], BF16, name="ones_b")
+        nc.vector.memset(ones_b[:], 1.0)
+        rows_sb = const.tile([P, P], BF16, name="rows_sb")
+        nc.vector.memset(rows_sb[:], 0.0)
+        nc.scalar.dma_start(out=rows_sb[0:D_TILES, :], in_=b1.rearrange("(t p) -> t p", p=P))
+        nc.scalar.dma_start(out=rows_sb[D_TILES : D_TILES + N_TILES, :], in_=b2.rearrange("(t p) -> t p", p=P))
         gamma_b = const.tile([P, D], BF16, name="gamma_b")
-        nc.scalar.dma_start(out=gamma_b[:], in_=gamma.partition_broadcast(P))
         beta_b = const.tile([P, D], BF16, name="beta_b")
-        nc.scalar.dma_start(out=beta_b[:], in_=beta.partition_broadcast(P))
+        bias_cols = const.tile([P, D_TILES + N_TILES], F32, name="bias_cols")
 
+        x_t = keep.tile([P, N_TILES, B], BF16, name="x_t")
         wt_codes = keep.tile([P, N_PASSES, D], U32, name="wt_codes", align_bytes=64)
         wt_scales = keep.tile([P, N_PASSES, D], U8, name="wt_scales", align_bytes=64)
-        w2_codes = keep.tile([P, D_PASSES, N], U32, name="w2_codes", align_bytes=64)
-        w2_scales = keep.tile([P, D_PASSES, N], U8, name="w2_scales", align_bytes=64)
-        x_sb = [keep.tile([P, N], BF16, name="x_sb%d" % bt) for bt in range(B_TILES)]
-        h_codes = [keep.tile([P, N_PASSES * P], U32, name="h_codes%d" % bt, align_bytes=64) for bt in range(B_TILES)]
-        h_scales = [keep.tile([P, N_PASSES * P], U8, name="h_scales%d" % bt, align_bytes=64) for bt in range(B_TILES)]
-        count = keep.tile([P, B_TILES], F32, name="count")
-        row_loss = keep.tile([P, B_TILES], F32, name="row_loss")
+        h_codes = keep.tile([P, N_PASSES, B], U32, name="h_codes", align_bytes=64)
+        h_scales = keep.tile([P, N_PASSES, B], U8, name="h_scales", align_bytes=64)
 
+        x_view = x.rearrange("(t p) n -> p t n", p=P)
+        m_view = drop_mask.rearrange("(t p) n -> p t n", p=P)
         w_view = W.rearrange("(t p) n -> p t n", p=P)
 
-        with tc.tile_pool(name="wstage", bufs=2) as stage:
-            w_nat = {}
-            xm_tiles = {}
+        w2_codes = {}
+        w2_scales = {}
+
+        w_again = {}
+        waiting = []
+        emitted = [0]
+
+        def later(call):
+            waiting.append(call)
+
+        def drain(keep_back):
+            while len(waiting) - emitted[0] > keep_back:
+                waiting[emitted[0]]()
+                emitted[0] += 1
+
+        def reload(j):
+            w_again[j] = again.tile([P, D_TILES, W2_CHUNK], BF16, name="w_again", tag="w_again")
+            nc.sync.dma_start(out=w_again[j][:], in_=w_view[:, :, j * W2_CHUNK : (j + 1) * W2_CHUNK])
+
+        def regroup_w2(j, gd, v_cols):
+            if gd == 0:
+                w2_codes[j] = ring.tile([P, D_PASSES, W2_CHUNK], U32, name="w2c", tag="w2c", align_bytes=64)
+                w2_scales[j] = ring.tile([P, D_PASSES, W2_CHUNK], U8, name="w2s", tag="w2s", align_bytes=64)
+            grouped = again.tile([P, W2_CHUNK, 4], BF16, name="w2g", tag="w2g", align_bytes=64)
+            for engine_copy, lo, hi in (
+                (nc.vector.tensor_copy, 0, v_cols),
+                (nc.scalar.copy, v_cols, W2_CHUNK),
+            ):
+                if hi > lo:
+                    engine_copy(
+                        out=grouped[:, lo:hi, :].rearrange("p (c i) t -> p c t i", i=4),
+                        in_=w_again[j][:, 4 * gd : 4 * gd + 4, lo:hi].rearrange("p t (c i) -> p c t i", i=4),
+                    )
+            later(
+                lambda: nc.vector.quantize_mx(
+                    out=w2_codes[j][:, gd, :].bitcast(FP8X4),
+                    scales=w2_scales[j][:, gd, :],
+                    in_=grouped[:].rearrange("p c t -> p (c t)"),
+                )
+            )
+
+        turn = [0]
+
+        def next_bank(count):
+            turn[0] = (turn[0] + 1) % count
+            return turn[0]
+
+        t_turn = [0]
+
+        def next_t_bank():
+            t_turn[0] = (t_turn[0] + 1) % 3
+            return 4 + t_turn[0]
+
+        acc1 = [bank_f32(4 + i) for i in range(4)]
+
+        def first_matmul(acc, d_tile, g):
+            d_cols = slice(P * d_tile, P * (d_tile + 1))
+            nc.tensor.matmul_mx(
+                out=acc[:],
+                lhsT=wt_codes[:, g, d_cols].bitcast(FP8X4),
+                lhsT_scale=wt_scales[:, g, d_cols],
+                rhs=h_codes[:, g, :].bitcast(FP8X4),
+                rhs_scale=h_scales[:, g, :],
+                start=(g == 0),
+                stop=(g == N_PASSES - 1),
+            )
+
+        def first_matmul_early(c):
+            for gl in range(CHUNK // K_PASS):
+                for i in range(4):
+                    first_matmul(acc1[i], i, c * (CHUNK // K_PASS) + gl)
+
+        with tc.tile_pool(name="stage", bufs=2) as stage:
+            x_in = {}
+            m_in = {}
+            w_in = {}
 
             def load(c):
-                w_nat[c] = stage.tile([P, D_TILES, CHUNK], BF16, name="w_nat", tag="w_nat")
-                nc.sync.dma_start(out=w_nat[c][:], in_=w_view[:, :, c * CHUNK : (c + 1) * CHUNK])
-                nc.sync.dma_start(out=x_sb[c][:], in_=x[c * P : (c + 1) * P, :])
-                xm_tiles[c] = stage.tile([P, N], BF16, name="mask", tag="mask")
-                nc.sync.dma_start(out=xm_tiles[c][:], in_=drop_mask[c * P : (c + 1) * P, :])
+                cols = slice(c * CHUNK, (c + 1) * CHUNK)
+                x_in[c] = stage.tile([P, B_TILES, CHUNK], BF16, name="x_in", tag="x_in")
+                nc.sync.dma_start(out=x_in[c][:], in_=x_view[:, :, cols])
+                m_in[c] = stage.tile([P, B_TILES, CHUNK], BF16, name="m_in", tag="m_in")
+                nc.sync.dma_start(out=m_in[c][:], in_=m_view[:, :, cols])
+                w_in[c] = stage.tile([P, D_TILES, CHUNK], BF16, name="w_in", tag="w_in")
+                nc.sync.dma_start(out=w_in[c][:], in_=w_view[:, :, cols])
 
-            def prepare_w_first(c):
-                wn = w_nat[c]
+            def mask_x(c):
+                nc.vector.tensor_tensor(out=m_in[c][:], in0=x_in[c][:], in1=m_in[c][:], op=ALU.mult)
+
+            def transpose_x(c):
+                xc = x_in[c]
+                for pair in range(CHUNK // (2 * P)):
+                    bk = bank_bf16(next_bank(4))
+                    for half in range(2):
+                        first = P * (2 * pair + half)
+                        for bt in range(B_TILES):
+                            nc.tensor.transpose(
+                                bk[:, B * half + P * bt : B * half + P * (bt + 1)], xc[:, bt, first : first + P], ident_b[:]
+                            )
+                    nt0 = (CHUNK // P) * c + 2 * pair
+                    dst = x_t[:, nt0 : nt0 + 2, :].rearrange("p a b -> p (a b)")
+                    if pair % 2 == 0:
+                        nc.vector.tensor_copy(out=dst, in_=bk[:])
+                    else:
+                        nc.scalar.copy(out=dst, in_=bk[:])
+                    drain(1)
+
+            def scale_and_quantise_h(g, h_words):
+                grouped = stage.tile([P, 4 * B], BF16, name="hg", tag="hg", align_bytes=64)
+                nc.vector.tensor_scalar_mul(out=grouped[:], in0=h_words[:].bitcast(BF16), scalar1=KEEP_SCALE)
+                later(
+                    lambda: nc.vector.quantize_mx(
+                        out=h_codes[:, g, :].bitcast(FP8X4), scales=h_scales[:, g, :], in_=grouped[:]
+                    )
+                )
+
+            def prepare_h(c):
+                xm = m_in[c]
+                for gl in range(CHUNK // K_PASS):
+                    g = c * (CHUNK // K_PASS) + gl
+                    h_words = stage.tile([P, 2 * B], F32, name="h_words", tag="h_words")
+                    hw_view = h_words[:].rearrange("p (c u) -> p c u", u=2)
+                    for pr in range(B_TILES // 2):
+                        bk = bank_f32(next_bank(4))
+                        planes = bk[:].rearrange("p (u c) -> p u c", u=2)
+                        for bl in range(2):
+                            words = xm[:, 2 * pr + bl, :].bitcast(F32)
+                            for u in range(2):
+                                first = 256 * gl + P * u
+                                nc.tensor.transpose(
+                                    planes[:, u, P * bl : P * (bl + 1)], words[:, first : first + P], ident_f[:]
+                                )
+                        nc.scalar.copy(
+                            out=hw_view[:, 256 * pr : 256 * (pr + 1), :], in_=bk[:].rearrange("p (u c) -> p c u", u=2)
+                        )
+                    drain(1)
+                    later(lambda g=g, h_words=h_words: scale_and_quantise_h(g, h_words))
+
+            def quantise_wt(g, half, grouped):
+                cols = slice(BANK_F32 * half, BANK_F32 * (half + 1))
+                nc.vector.quantize_mx(out=wt_codes[:, g, cols].bitcast(FP8X4), scales=wt_scales[:, g, cols], in_=grouped[:])
+
+            def prepare_w_first(c, share):
+                wn = w_in[c]
                 for gl in range(CHUNK // K_PASS):
                     g = c * (CHUNK // K_PASS) + gl
                     for half in range(2):
-                        grouped = stage.tile([P, 4 * N_TILE], BF16, name="wtg", tag="wtg", bufs=3, align_bytes=64)
+                        grouped = stage.tile([P, 4 * BANK_F32], BF16, name="wtg", tag="wtg", bufs=3, align_bytes=64)
                         g_words = grouped[:].bitcast(F32).rearrange("p (c u) -> p c u", u=2)
                         for j in range(2):
-                            bank = psum_t.tile([P, N_TILE], F32, name="bank", tag="tp")
-                            planes = bank[:].rearrange("p (u c) -> p u c", u=2)
+                            bk = bank_f32(next_bank(4))
+                            planes = bk[:].rearrange("p (u c) -> p u c", u=2)
                             for dd in range(2):
-                                d_tile = 4 * half + 2 * j + dd
-                                words = wn[:, d_tile, :].bitcast(F32)
+                                words = wn[:, 4 * half + 2 * j + dd, :].bitcast(F32)
                                 for u in range(2):
                                     first = 256 * gl + P * u
                                     nc.tensor.transpose(
                                         planes[:, u, P * dd : P * (dd + 1)], words[:, first : first + P], ident_f[:]
                                     )
-                            nc.scalar.copy(
-                                out=g_words[:, 256 * j : 256 * (j + 1), :],
-                                in_=bank[:].rearrange("p (u c) -> p c u", u=2),
-                            )
-                        cols = slice(N_TILE * half, N_TILE * (half + 1))
-                        nc.vector.quantize_mx(
-                            out=wt_codes[:, g, cols].bitcast(FP8X4), scales=wt_scales[:, g, cols], in_=grouped[:]
-                        )
-
-            def prepare_w_second(c):
-                wn = w_nat[c]
-                for gd in range(D_PASSES):
-                    for blk in range(CHUNK // N_TILE):
-                        grouped = stage.tile([P, N_TILE, 4], BF16, name="w2g", tag="w2g", bufs=3, align_bytes=64)
-                        first = N_TILE * blk
-                        for engine_copy, lo, hi in (
-                            (nc.vector.tensor_copy, 0, VECTOR_COLS),
-                            (nc.scalar.copy, VECTOR_COLS, N_TILE),
-                        ):
+                            engine_copy = nc.vector.tensor_copy if (share and j == 1) else nc.scalar.copy
                             engine_copy(
-                                out=grouped[:, lo:hi, :].rearrange("p (c i) t -> p c t i", i=4),
-                                in_=wn[:, 4 * gd : 4 * gd + 4, first + lo : first + hi].rearrange(
-                                    "p t (c i) -> p c t i", i=4
-                                ),
+                                out=g_words[:, 256 * j : 256 * (j + 1), :], in_=bk[:].rearrange("p (u c) -> p c u", u=2)
                             )
-                        cols = slice(c * CHUNK + first, c * CHUNK + first + N_TILE)
-                        nc.vector.quantize_mx(
-                            out=w2_codes[:, gd, cols].bitcast(FP8X4),
-                            scales=w2_scales[:, gd, cols],
-                            in_=grouped[:].rearrange("p c t -> p (c t)"),
-                        )
-
-            def prepare_h(bt):
-                xm = xm_tiles[bt]
-                nc.vector.tensor_tensor(out=xm[:], in0=x_sb[bt][:], in1=xm[:], op=ALU.mult)
-                words = xm[:].bitcast(F32)
-                grouped = stage.tile([P, 4 * N_PASSES * P], BF16, name="hg", tag="hg", bufs=1, align_bytes=64)
-                g_view = grouped[:].rearrange("p (c u e) -> p c u e", u=2, e=2)
-                for j in range(N_PASSES // 2):
-                    bank = psum_t.tile([P, N_TILE], F32, name="bank", tag="tp")
-                    planes = bank[:].rearrange("p (u c) -> p u c", u=2)
-                    for gl in range(2):
-                        for u in range(2):
-                            first = 256 * (2 * j + gl) + P * u
-                            nc.tensor.transpose(
-                                planes[:, u, P * gl : P * (gl + 1)], words[:, first : first + P], ident_f[:]
-                            )
-                    nc.scalar.activation(
-                        out=g_view[:, 256 * j : 256 * (j + 1), :, :],
-                        in_=bank[:].bitcast(BF16).rearrange("p (u c e) -> p c u e", u=2, e=2),
-                        func=ACT.Copy,
-                        scale=KEEP_SCALE,
-                    )
-                nc.vector.quantize_mx(out=h_codes[bt][:].bitcast(FP8X4), scales=h_scales[bt][:], in_=grouped[:])
+                        drain(1)
+                        later(lambda g=g, half=half, grouped=grouped: quantise_wt(g, half, grouped))
 
             load(0)
             load(1)
+            mask_x(0)
             for c in range(CHUNKS):
-                prepare_w_first(c)
-                prepare_w_second(c)
+                transpose_x(c)
                 prepare_h(c)
+                if c >= 1:
+                    first_matmul_early(c - 1)
+                if c + 1 < CHUNKS:
+                    mask_x(c + 1)
+                prepare_w_first(c, c == CHUNKS - 1)
                 if c + 2 < CHUNKS:
                     load(c + 2)
+            reload(0)
+            reload(1)
+            nc.sync.dma_start(out=gamma_b[:], in_=gamma.partition_broadcast(P))
+            nc.sync.dma_start(out=beta_b[:], in_=beta.partition_broadcast(P))
+            bk = bank_bf16(next_bank(4))
+            nc.tensor.transpose(bk[:, 0:P], rows_sb[:], ident_b[:])
+            nc.vector.tensor_copy(out=bias_cols[:], in_=bk[:, 0 : D_TILES + N_TILES])
+            drain(0)
+            first_matmul_early(CHUNKS - 1)
 
         with tc.tile_pool(name="post", bufs=2) as post, tc.tile_pool(name="small", bufs=2) as small:
-            for bt in range(B_TILES):
-                rows = slice(bt * P, (bt + 1) * P)
-                xt = x_sb[bt]
+            enc_t = post.tile([P, D_TILES, B], F32, name="enc_t", tag="enc_t", bufs=1)
+            e_codes = post.tile([P, D_PASSES, B], U32, name="e_codes", tag="e_codes", bufs=1, align_bytes=64)
+            e_scales = post.tile([P, D_PASSES, B], U8, name="e_scales", tag="e_scales", bufs=1, align_bytes=64)
 
-                nz = post.tile([P, N], BF16, name="nz", tag="nz", bufs=1)
-                nc.vector.tensor_single_scalar(out=nz[:], in_=xt[:], scalar=0.0, op=ALU.not_equal)
-                nc.scalar.activation(out=nz[:], in_=nz[:], func=ACT.Copy, accum_out=count[:, bt : bt + 1])
-
-                pre = post.tile([P, D], F32, name="pre", tag="pre")
-                for half in range(D // N_TILE):
-                    cols = slice(N_TILE * half, N_TILE * (half + 1))
-                    acc = psum_1.tile([P, N_TILE], F32, name="acc1", tag="acc1")
-                    for g in range(N_PASSES):
-                        m_cols = slice(P * g, P * (g + 1))
-                        nc.tensor.matmul_mx(
-                            out=acc[:],
-                            lhsT=h_codes[bt][:, m_cols].bitcast(FP8X4),
-                            lhsT_scale=h_scales[bt][:, m_cols],
-                            rhs=wt_codes[:, g, cols].bitcast(FP8X4),
-                            rhs_scale=wt_scales[:, g, cols],
-                            start=(g == 0),
-                            stop=(g == N_PASSES - 1),
-                        )
-                    nc.vector.tensor_tensor(out=pre[:, cols], in0=acc[:], in1=b1_b[:, cols], op=ALU.add)
-                enc = post.tile([P, D], F32, name="enc", tag="enc")
-                enc_sum = small.tile([P, 1], F32, name="enc_sum", tag="enc_sum")
-                nc.scalar.activation(out=enc[:], in_=pre[:], func=ACT.Tanh, accum_out=enc_sum[:])
-                enc_bf = post.tile([P, D], BF16, name="enc_bf", tag="enc_bf")
-                nc.scalar.activation(out=enc_bf[:], in_=pre[:], func=ACT.Tanh)
-
-                bank = psum_t.tile([P, D], BF16, name="bank_b", tag="tp")
-                for d_tile in range(D_TILES):
-                    d_cols = slice(P * d_tile, P * (d_tile + 1))
-                    nc.tensor.transpose(bank[:, d_cols], enc_bf[:, d_cols], ident_b[:])
-                grouped = post.tile([P, D], BF16, name="eg", tag="eg", align_bytes=64)
-                nc.scalar.copy(
-                    out=grouped[:].rearrange("p (g r t) -> p g r t", g=D_PASSES, t=4),
-                    in_=bank[:].rearrange("p (g t r) -> p g r t", g=D_PASSES, t=4),
+            def tanh(acc, d_tile):
+                nc.scalar.activation(
+                    out=enc_t[:, d_tile, :], in_=acc[:], func=ACT.Tanh, bias=bias_cols[:, d_tile : d_tile + 1]
                 )
-                e_codes = post.tile([P, D_PASSES * P], U32, name="e_codes", tag="e_codes", align_bytes=64)
-                e_scales = post.tile([P, D_PASSES * P], U8, name="e_scales", tag="e_scales", align_bytes=64)
-                nc.vector.quantize_mx(out=e_codes[:].bitcast(FP8X4), scales=e_scales[:], in_=grouped[:])
 
+            def regroup_enc(gd, v_cols):
+                grouped = post.tile([P, B, 4], BF16, name="eg", tag="eg", align_bytes=64)
+                for engine_copy, lo, hi in ((nc.vector.tensor_copy, 0, v_cols), (nc.scalar.copy, v_cols, B)):
+                    if hi > lo:
+                        engine_copy(
+                            out=grouped[:, lo:hi, :], in_=enc_t[:, 4 * gd : 4 * gd + 4, lo:hi].rearrange("p t b -> p b t")
+                        )
+                later(
+                    lambda: nc.vector.quantize_mx(
+                        out=e_codes[:, gd, :].bitcast(FP8X4),
+                        scales=e_scales[:, gd, :],
+                        in_=grouped[:].rearrange("p b t -> p (b t)"),
+                    )
+                )
+
+            ln = {}
+
+            def ln_transpose(bt):
+                b_cols = slice(P * bt, P * (bt + 1))
+                enc = post.tile([P, D], F32, name="enc", tag="enc")
+                part_sum = small.tile([P, 2], F32, name="part_sum", tag="part_sum")
+                for dh in range(2):
+                    bk = bank_f32(next_t_bank())
+                    for i in range(4):
+                        nc.tensor.transpose(bk[:, P * i : P * (i + 1)], enc_t[:, 4 * dh + i, b_cols], ident_f[:])
+                    nc.scalar.activation(
+                        out=enc[:, BANK_F32 * dh : BANK_F32 * (dh + 1)],
+                        in_=bk[:],
+                        func=ACT.Copy,
+                        accum_out=part_sum[:, dh : dh + 1],
+                    )
+                ln[bt] = {"enc": enc, "part_sum": part_sum}
+
+            def ln_mean(bt):
+                t = ln[bt]
+                enc_sum = small.tile([P, 1], F32, name="enc_sum", tag="enc_sum")
+                nc.vector.tensor_tensor(out=enc_sum[:], in0=t["part_sum"][:, 0:1], in1=t["part_sum"][:, 1:2], op=ALU.add)
                 neg_mean = small.tile([P, 1], F32, name="neg_mean", tag="neg_mean")
                 nc.vector.tensor_scalar_mul(out=neg_mean[:], in0=enc_sum[:], scalar1=-1.0 / D)
+                t["neg_mean"] = neg_mean
+
+            def ln_square(bt):
+                t = ln[bt]
+                fin = post.tile([P, D], F32, name="fin", tag="fin")
                 sq_sum = small.tile([P, 1], F32, name="sq_sum", tag="sq_sum")
-                nc.scalar.activation(out=pre[:], in_=enc[:], func=ACT.Square, bias=neg_mean[:], accum_out=sq_sum[:])
+                nc.scalar.activation(
+                    out=fin[:], in_=t["enc"][:], func=ACT.Square, bias=t["neg_mean"][:], accum_out=sq_sum[:]
+                )
+                t["fin"] = fin
+                t["sq_sum"] = sq_sum
+
+            def ln_rstd(bt):
+                t = ln[bt]
                 var_eps = small.tile([P, 1], F32, name="var_eps", tag="var_eps")
                 nc.vector.tensor_scalar(
-                    out=var_eps[:], in0=sq_sum[:], scalar1=1.0 / D, scalar2=LN_EPS, op0=ALU.mult, op1=ALU.add
+                    out=var_eps[:], in0=t["sq_sum"][:], scalar1=1.0 / D, scalar2=LN_EPS, op0=ALU.mult, op1=ALU.add
                 )
                 rstd = small.tile([P, 1], F32, name="rstd", tag="rstd")
                 nc.gpsimd.tensor_tensor(out=rstd[:], in0=var_eps[:], in1=neg_half[:], op=ALU.pow)
-                fin = post.tile([P, D], F32, name="fin", tag="fin")
-                nc.vector.scalar_tensor_tensor(
-                    out=fin[:], in0=enc[:], scalar=neg_mean[:], in1=gamma_b[:], op0=ALU.add, op1=ALU.mult
-                )
-                nc.vector.scalar_tensor_tensor(
-                    out=fin[:], in0=fin[:], scalar=rstd[:], in1=beta_b[:], op0=ALU.mult, op1=ALU.add
-                )
-                nc.sync.dma_start(out=out_0[rows, :], in_=fin[:])
+                t["rstd"] = rstd
 
-                tile_loss = small.tile([P, N // N_TILE], F32, name="tile_loss", tag="tile_loss")
-                for nt in range(N // N_TILE):
-                    cols = slice(N_TILE * nt, N_TILE * (nt + 1))
-                    x_less_b2 = post.tile([P, N_TILE], F32, name="xb", tag="xb", bufs=3)
-                    nc.vector.tensor_tensor(out=x_less_b2[:], in0=xt[:, cols], in1=b2_b[:, cols], op=ALU.subtract)
-                    acc = psum_2.tile([P, N_TILE], F32, name="acc2", tag="acc2")
-                    for gd in range(D_PASSES):
-                        m_cols = slice(P * gd, P * (gd + 1))
-                        nc.tensor.matmul_mx(
-                            out=acc[:],
-                            lhsT=e_codes[:, m_cols].bitcast(FP8X4),
-                            lhsT_scale=e_scales[:, m_cols],
-                            rhs=w2_codes[:, gd, cols].bitcast(FP8X4),
-                            rhs_scale=w2_scales[:, gd, cols],
-                            start=(gd == 0),
-                            stop=(gd == D_PASSES - 1),
-                        )
-                    diff = post.tile([P, N_TILE], F32, name="diff", tag="diff", bufs=3)
-                    nc.vector.tensor_tensor(out=diff[:], in0=acc[:], in1=x_less_b2[:], op=ALU.subtract)
-                    nc.vector.scalar_tensor_tensor(
-                        out=diff[:], in0=xt[:, cols], scalar=0.0, in1=diff[:], op0=ALU.not_equal, op1=ALU.mult
+            def ln_final(bt):
+                t = ln[bt]
+                fin = t["fin"]
+                nc.vector.scalar_tensor_tensor(
+                    out=fin[:], in0=t["enc"][:], scalar=t["neg_mean"][:], in1=gamma_b[:], op0=ALU.add, op1=ALU.mult
+                )
+                nc.vector.scalar_tensor_tensor(
+                    out=fin[:], in0=fin[:], scalar=t["rstd"][:], in1=beta_b[:], op0=ALU.mult, op1=ALU.add
+                )
+                nc.sync.dma_start(out=out_0[P * bt : P * (bt + 1), :], in_=fin[:])
+
+            squares = {}
+            not_zero = {}
+
+            def difference(j, ntl):
+                nt = 4 * j + ntl
+                n_cols = slice(P * ntl, P * (ntl + 1))
+                acc = bank_f32(next_bank(4))
+                for gd in range(D_PASSES):
+                    nc.tensor.matmul_mx(
+                        out=acc[:],
+                        lhsT=w2_codes[j][:, gd, n_cols].bitcast(FP8X4),
+                        lhsT_scale=w2_scales[j][:, gd, n_cols],
+                        rhs=e_codes[:, gd, :].bitcast(FP8X4),
+                        rhs_scale=e_scales[:, gd, :],
+                        start=(gd == 0),
+                        stop=(gd == D_PASSES - 1),
                     )
-                    nc.scalar.activation(out=diff[:], in_=diff[:], func=ACT.Square, accum_out=tile_loss[:, nt : nt + 1])
-                nc.vector.tensor_reduce(out=row_loss[:, bt : bt + 1], in_=tile_loss[:], axis=AXIS_X, op=ALU.add)
+                nc.vector.scalar_tensor_tensor(
+                    out=squares[j][:, ntl, :],
+                    in0=acc[:],
+                    scalar=bias_cols[:, D_TILES + nt : D_TILES + nt + 1],
+                    in1=x_t[:, nt, :],
+                    op0=ALU.add,
+                    op1=ALU.subtract,
+                )
 
+            def mask_difference(j, lo, hi):
+                flat = squares[j][:, lo:hi, :].rearrange("p a b -> p (a b)")
+                x_flat = x_t[:, 4 * j + lo : 4 * j + hi, :].rearrange("p a b -> p (a b)")
+                nc.vector.scalar_tensor_tensor(out=flat, in0=x_flat, scalar=0.0, in1=flat, op0=ALU.not_equal, op1=ALU.mult)
+
+            def row_sums(j, lo, hi, col):
+                for bt in range(B_TILES):
+                    bk = bank_f32(next_t_bank())
+                    for ntl in range(lo, hi):
+                        nc.tensor.transpose(
+                            bk[:, P * (ntl - lo) : P * (ntl - lo + 1)], squares[j][:, ntl, P * bt : P * (bt + 1)], ident_f[:]
+                        )
+                    nc.scalar.activation(
+                        out=junk[:, 0 : P * (hi - lo)],
+                        in_=bk[:, 0 : P * (hi - lo)],
+                        func=ACT.Square,
+                        accum_out=loss_cols[:, bt, col : col + 1],
+                    )
+
+            def mark_not_zero(j):
+                not_zero[j] = post.tile([P, 4, B], BF16, name="nz", tag="nz")
+                nc.vector.tensor_single_scalar(
+                    out=not_zero[j][:].rearrange("p a b -> p (a b)"),
+                    in_=x_t[:, 4 * j : 4 * j + 4, :].rearrange("p a b -> p (a b)"),
+                    scalar=0.0,
+                    op=ALU.not_equal,
+                )
+
+            def count(j):
+                for ntl in range(4):
+                    nt = 4 * j + ntl
+                    nc.tensor.matmul(
+                        out=counts[:], lhsT=ones_b[:], rhs=not_zero[j][:, ntl, :], start=(nt == 0), stop=(nt == N_TILES - 1)
+                    )
+
+            junk = post.tile([P, BANK_F32], BF16, name="junk", tag="junk", bufs=1)
+            loss_cols = post.tile([P, B_TILES, LOSS_COLS], F32, name="loss_cols", tag="loss_cols", bufs=1)
+
+            for i in range(4):
+                tanh(acc1[i], i)
+            for i in range(4):
+                if i < WINDOW_CHUNKS:
+                    regroup_w2(i, 0, V_COLS_WINDOW)
+                    drain(1)
+                    regroup_w2(i, 1, V_COLS_WINDOW)
+                    drain(1)
+                    reload(i + 2)
+                if i == 0:
+                    regroup_enc(0, B)
+                    drain(1)
+                acc = bank_f32(i)
+                for g in range(N_PASSES):
+                    first_matmul(acc, 4 + i, g)
+                tanh(acc, 4 + i)
+            drain(0)
+            regroup_enc(1, B // 2)
+            drain(0)
+            counts = bank_f32(COUNT_BANK)
+            ln_transpose(0)
+
+            last = W2_CHUNKS - 1
+            for j in range(last):
+                squares[j] = post.tile([P, 4, B], F32, name="diff", tag="diff", bufs=3)
+                for ntl in range(4):
+                    difference(j, ntl)
+                if 1 <= j <= B_TILES:
+                    ln_rstd(j - 1)
+                mask_difference(j, 0, 4)
+                if j >= 1:
+                    row_sums(j - 1, 0, 4, j - 1)
+                    count(j - 1)
+                if 1 <= j <= B_TILES:
+                    ln_final(j - 1)
+                if j < B_TILES:
+                    ln_mean(j)
+                    ln_square(j)
+                mark_not_zero(j)
+                drain(0)
+                if j + 1 < B_TILES:
+                    ln_transpose(j + 1)
+                coming = j + WINDOW_CHUNKS
+                if coming < W2_CHUNKS:
+                    regroup_w2(coming, 0, V_COLS_LOOP)
+                    regroup_w2(coming, 1, V_COLS_LOOP)
+                    if coming + 2 < W2_CHUNKS:
+                        reload(coming + 2)
+
+            squares[last] = post.tile([P, 4, B], F32, name="diff", tag="diff", bufs=3)
+            mark_not_zero(last)
+            difference(last, 0)
+            difference(last, 1)
+            mask_difference(last, 0, 2)
+            difference(last, 2)
+            difference(last, 3)
+            row_sums(last - 1, 0, 4, last - 1)
+            count(last - 1)
+            count(last)
+            mask_difference(last, 2, 4)
+            row_sums(last, 0, 2, last)
+            counts_sb = post.tile([P, B], F32, name="counts_sb", tag="counts_sb", bufs=1)
+            nc.vector.tensor_copy(out=counts_sb[:], in_=counts[:])
+            bk = bank_f32(next_bank(4))
+            for bt in range(B_TILES):
+                nc.tensor.transpose(bk[:, P * bt : P * (bt + 1)], counts_sb[:, P * bt : P * (bt + 1)], ident_f[:])
             inv_count = small.tile([P, B_TILES], F32, name="inv_count", tag="inv_count")
-            nc.vector.reciprocal(out=inv_count[:], in_=count[:])
+            nc.vector.reciprocal(
+                out=inv_count[:].rearrange("p (a c) -> p a c", c=1), in_=bk[:].rearrange("p (a c) -> p a c", c=P)[:, :, 0:1]
+            )
+            row_sums(last, 2, 4, last + 1)
+
+            totals = small.tile([P, B_TILES], F32, name="totals", tag="totals")
+            nc.vector.tensor_reduce(out=totals[:], in_=loss_cols[:], axis=AXIS_X, op=ALU.add)
             per_row = small.tile([P, B_TILES], F32, name="per_row", tag="per_row")
-            nc.vector.tensor_tensor(out=per_row[:], in0=row_loss[:], in1=inv_count[:], op=ALU.mult)
+            nc.vector.tensor_tensor(out=per_row[:], in0=totals[:], in1=inv_count[:], op=ALU.mult)
             nc.vector.tensor_reduce(out=spread[:, 0:1], in_=per_row[:], axis=AXIS_X, op=ALU.add)
-            bank = psum_t.tile([P, N_TILE], F32, name="bank", tag="tp")
-            nc.tensor.transpose(bank[:, 0:P], spread[:], ident_f[:])
+            bk = bank_f32(next_bank(4))
+            nc.tensor.transpose(bk[:, 0:P], spread[:], ident_f[:])
             total = small.tile([P, 1], F32, name="total", tag="total")
-            nc.vector.tensor_reduce(out=total[:], in_=bank[:, 0:P], axis=AXIS_X, op=ALU.add)
+            nc.vector.tensor_reduce(out=total[:], in_=bk[:, 0:P], axis=AXIS_X, op=ALU.add)
             nc.sync.dma_start(out=out_1.rearrange("(a b) -> a b", a=1), in_=total[0:1, 0:1])

@@ -21,8 +21,9 @@ CHUNK = 1024
 CHUNKS = N // CHUNK
 W2_CHUNK = 512
 W2_CHUNKS = N // W2_CHUNK
-RING = 4
-WINDOW_CHUNKS = 3
+RING = 6
+ORDER = (6, 7, 0, 1, 2, 3, 4, 5)
+V_COLS_TAIL = 256
 V_COLS_WINDOW = 320
 V_COLS_LOOP = 0
 COUNT_BANK = 7
@@ -44,9 +45,7 @@ def tile_multipleembedding_kernel(tc, x, drop_mask, W, b1, b2, gamma, beta, out_
         const = ctx.enter_context(tc.tile_pool(name="const", bufs=1))
         keep = ctx.enter_context(tc.tile_pool(name="keep", bufs=1))
         ring = ctx.enter_context(tc.tile_pool(name="ring", bufs=RING))
-        again = ctx.enter_context(tc.tile_pool(name="again", bufs=2))
         psum = ctx.enter_context(tc.psum_pool(name="psum", bufs=1))
-        ctx.enter_context(tc.manual_schedule())
 
         def bank_f32(k):
             return psum.tile([P, BANK_F32], F32, name="bank%d" % k, tag="bank%d" % k)
@@ -101,11 +100,11 @@ def tile_multipleembedding_kernel(tc, x, drop_mask, W, b1, b2, gamma, beta, out_
             w_again[j] = again.tile([P, D_TILES, W2_CHUNK], BF16, name="w_again", tag="w_again")
             nc.sync.dma_start(out=w_again[j][:], in_=w_view[:, :, j * W2_CHUNK : (j + 1) * W2_CHUNK])
 
-        def regroup_w2(j, gd, v_cols):
+        def regroup_w2(pool, w_rows, first, j, gd, v_cols):
             if gd == 0:
                 w2_codes[j] = ring.tile([P, D_PASSES, W2_CHUNK], U32, name="w2c", tag="w2c", align_bytes=64)
                 w2_scales[j] = ring.tile([P, D_PASSES, W2_CHUNK], U8, name="w2s", tag="w2s", align_bytes=64)
-            grouped = again.tile([P, W2_CHUNK, 4], BF16, name="w2g", tag="w2g", align_bytes=64)
+            grouped = pool.tile([P, W2_CHUNK, 4], BF16, name="w2g", tag="w2g", bufs=2, align_bytes=64)
             for engine_copy, lo, hi in (
                 (nc.vector.tensor_copy, 0, v_cols),
                 (nc.scalar.copy, v_cols, W2_CHUNK),
@@ -113,7 +112,7 @@ def tile_multipleembedding_kernel(tc, x, drop_mask, W, b1, b2, gamma, beta, out_
                 if hi > lo:
                     engine_copy(
                         out=grouped[:, lo:hi, :].rearrange("p (c i) t -> p c t i", i=4),
-                        in_=w_again[j][:, 4 * gd : 4 * gd + 4, lo:hi].rearrange("p t (c i) -> p c t i", i=4),
+                        in_=w_rows[:, 4 * gd : 4 * gd + 4, first + lo : first + hi].rearrange("p t (c i) -> p c t i", i=4),
                     )
             later(
                 lambda: nc.vector.quantize_mx(
@@ -135,7 +134,6 @@ def tile_multipleembedding_kernel(tc, x, drop_mask, W, b1, b2, gamma, beta, out_
             t_turn[0] = (t_turn[0] + 1) % 3
             return 4 + t_turn[0]
 
-        acc1 = [bank_f32(4 + i) for i in range(4)]
 
         def first_matmul(acc, d_tile, g):
             d_cols = slice(P * d_tile, P * (d_tile + 1))
@@ -148,11 +146,6 @@ def tile_multipleembedding_kernel(tc, x, drop_mask, W, b1, b2, gamma, beta, out_
                 start=(g == 0),
                 stop=(g == N_PASSES - 1),
             )
-
-        def first_matmul_early(c):
-            for gl in range(CHUNK // K_PASS):
-                for i in range(4):
-                    first_matmul(acc1[i], i, c * (CHUNK // K_PASS) + gl)
 
         with tc.tile_pool(name="stage", bufs=2) as stage:
             x_in = {}
@@ -174,7 +167,7 @@ def tile_multipleembedding_kernel(tc, x, drop_mask, W, b1, b2, gamma, beta, out_
             def transpose_x(c):
                 xc = x_in[c]
                 for pair in range(CHUNK // (2 * P)):
-                    bk = bank_bf16(next_bank(4))
+                    bk = bank_bf16(next_bank(8))
                     for half in range(2):
                         first = P * (2 * pair + half)
                         for bt in range(B_TILES):
@@ -205,7 +198,7 @@ def tile_multipleembedding_kernel(tc, x, drop_mask, W, b1, b2, gamma, beta, out_
                     h_words = stage.tile([P, 2 * B], F32, name="h_words", tag="h_words")
                     hw_view = h_words[:].rearrange("p (c u) -> p c u", u=2)
                     for pr in range(B_TILES // 2):
-                        bk = bank_f32(next_bank(4))
+                        bk = bank_f32(next_bank(8))
                         planes = bk[:].rearrange("p (u c) -> p u c", u=2)
                         for bl in range(2):
                             words = xm[:, 2 * pr + bl, :].bitcast(F32)
@@ -232,7 +225,7 @@ def tile_multipleembedding_kernel(tc, x, drop_mask, W, b1, b2, gamma, beta, out_
                         grouped = stage.tile([P, 4 * BANK_F32], BF16, name="wtg", tag="wtg", bufs=3, align_bytes=64)
                         g_words = grouped[:].bitcast(F32).rearrange("p (c u) -> p c u", u=2)
                         for j in range(2):
-                            bk = bank_f32(next_bank(4))
+                            bk = bank_f32(next_bank(8))
                             planes = bk[:].rearrange("p (u c) -> p u c", u=2)
                             for dd in range(2):
                                 words = wn[:, 4 * half + 2 * j + dd, :].bitcast(F32)
@@ -254,24 +247,24 @@ def tile_multipleembedding_kernel(tc, x, drop_mask, W, b1, b2, gamma, beta, out_
             for c in range(CHUNKS):
                 transpose_x(c)
                 prepare_h(c)
-                if c >= 1:
-                    first_matmul_early(c - 1)
                 if c + 1 < CHUNKS:
                     mask_x(c + 1)
                 prepare_w_first(c, c == CHUNKS - 1)
                 if c + 2 < CHUNKS:
                     load(c + 2)
-            reload(0)
-            reload(1)
-            nc.sync.dma_start(out=gamma_b[:], in_=gamma.partition_broadcast(P))
-            nc.sync.dma_start(out=beta_b[:], in_=beta.partition_broadcast(P))
-            bk = bank_bf16(next_bank(4))
+            bk = bank_bf16(next_bank(8))
             nc.tensor.transpose(bk[:, 0:P], rows_sb[:], ident_b[:])
             nc.vector.tensor_copy(out=bias_cols[:], in_=bk[:, 0 : D_TILES + N_TILES])
+            drain(1)
+            for j in ORDER[0:2]:
+                for gd in range(D_PASSES):
+                    regroup_w2(stage, w_in[CHUNKS - 1], W2_CHUNK * (j % 2), j, gd, V_COLS_TAIL)
+                    drain(1)
             drain(0)
-            first_matmul_early(CHUNKS - 1)
 
-        with tc.tile_pool(name="post", bufs=2) as post, tc.tile_pool(name="small", bufs=2) as small:
+        with tc.tile_pool(name="again", bufs=2) as again, tc.tile_pool(name="post", bufs=2) as post, tc.tile_pool(
+            name="small", bufs=2
+        ) as small:
             enc_t = post.tile([P, D_TILES, B], F32, name="enc_t", tag="enc_t", bufs=1)
             e_codes = post.tile([P, D_PASSES, B], U32, name="e_codes", tag="e_codes", bufs=1, align_bytes=64)
             e_scales = post.tile([P, D_PASSES, B], U8, name="e_scales", tag="e_scales", bufs=1, align_bytes=64)
@@ -407,32 +400,37 @@ def tile_multipleembedding_kernel(tc, x, drop_mask, W, b1, b2, gamma, beta, out_
                     op=ALU.not_equal,
                 )
 
-            def count(j):
+            def count(j, opening, closing):
                 for ntl in range(4):
-                    nt = 4 * j + ntl
                     nc.tensor.matmul(
-                        out=counts[:], lhsT=ones_b[:], rhs=not_zero[j][:, ntl, :], start=(nt == 0), stop=(nt == N_TILES - 1)
+                        out=counts[:],
+                        lhsT=ones_b[:],
+                        rhs=not_zero[j][:, ntl, :],
+                        start=(opening and ntl == 0),
+                        stop=(closing and ntl == 3),
                     )
 
             junk = post.tile([P, BANK_F32], BF16, name="junk", tag="junk", bufs=1)
             loss_cols = post.tile([P, B_TILES, LOSS_COLS], F32, name="loss_cols", tag="loss_cols", bufs=1)
 
-            for i in range(4):
-                tanh(acc1[i], i)
-            for i in range(4):
-                if i < WINDOW_CHUNKS:
-                    regroup_w2(i, 0, V_COLS_WINDOW)
-                    drain(1)
-                    regroup_w2(i, 1, V_COLS_WINDOW)
-                    drain(1)
-                    reload(i + 2)
-                if i == 0:
+            reload(0)
+            reload(1)
+            nc.sync.dma_start(out=gamma_b[:], in_=gamma.partition_broadcast(P))
+            nc.sync.dma_start(out=beta_b[:], in_=beta.partition_broadcast(P))
+            for d_tile in range(D_TILES):
+                j = d_tile // 2
+                gd = d_tile % 2
+                regroup_w2(again, w_again[j], 0, j, gd, V_COLS_WINDOW)
+                drain(1)
+                if gd == 1 and j + 2 < RING:
+                    reload(j + 2)
+                acc = bank_f32(d_tile % 4)
+                for g in range(N_PASSES):
+                    first_matmul(acc, d_tile, g)
+                tanh(acc, d_tile)
+                if d_tile == 4:
                     regroup_enc(0, B)
                     drain(1)
-                acc = bank_f32(i)
-                for g in range(N_PASSES):
-                    first_matmul(acc, 4 + i, g)
-                tanh(acc, 4 + i)
             drain(0)
             regroup_enc(1, B // 2)
             drain(0)
@@ -440,44 +438,44 @@ def tile_multipleembedding_kernel(tc, x, drop_mask, W, b1, b2, gamma, beta, out_
             ln_transpose(0)
 
             last = W2_CHUNKS - 1
-            for j in range(last):
+            for pos in range(last):
+                j = ORDER[pos]
                 squares[j] = post.tile([P, 4, B], F32, name="diff", tag="diff", bufs=3)
                 for ntl in range(4):
                     difference(j, ntl)
-                if 1 <= j <= B_TILES:
-                    ln_rstd(j - 1)
+                if 1 <= pos <= B_TILES:
+                    ln_rstd(pos - 1)
                 mask_difference(j, 0, 4)
-                if j >= 1:
-                    row_sums(j - 1, 0, 4, j - 1)
-                    count(j - 1)
-                if 1 <= j <= B_TILES:
-                    ln_final(j - 1)
-                if j < B_TILES:
-                    ln_mean(j)
-                    ln_square(j)
+                if pos >= 1:
+                    row_sums(ORDER[pos - 1], 0, 4, pos - 1)
+                    count(ORDER[pos - 1], pos == 1, False)
+                if 1 <= pos <= B_TILES:
+                    ln_final(pos - 1)
+                if pos < B_TILES:
+                    ln_mean(pos)
+                    ln_square(pos)
                 mark_not_zero(j)
                 drain(0)
-                if j + 1 < B_TILES:
-                    ln_transpose(j + 1)
-                coming = j + WINDOW_CHUNKS
-                if coming < W2_CHUNKS:
-                    regroup_w2(coming, 0, V_COLS_LOOP)
-                    regroup_w2(coming, 1, V_COLS_LOOP)
-                    if coming + 2 < W2_CHUNKS:
-                        reload(coming + 2)
+                if pos + 1 < B_TILES:
+                    ln_transpose(pos + 1)
+                if RING + pos < W2_CHUNKS:
+                    coming = ORDER[RING + pos]
+                    regroup_w2(again, w_again[coming], 0, coming, 0, V_COLS_LOOP)
+                    regroup_w2(again, w_again[coming], 0, coming, 1, V_COLS_LOOP)
 
-            squares[last] = post.tile([P, 4, B], F32, name="diff", tag="diff", bufs=3)
-            mark_not_zero(last)
-            difference(last, 0)
-            difference(last, 1)
-            mask_difference(last, 0, 2)
-            difference(last, 2)
-            difference(last, 3)
-            row_sums(last - 1, 0, 4, last - 1)
-            count(last - 1)
-            count(last)
-            mask_difference(last, 2, 4)
-            row_sums(last, 0, 2, last)
+            j = ORDER[last]
+            squares[j] = post.tile([P, 4, B], F32, name="diff", tag="diff", bufs=3)
+            mark_not_zero(j)
+            difference(j, 0)
+            difference(j, 1)
+            mask_difference(j, 0, 2)
+            difference(j, 2)
+            difference(j, 3)
+            row_sums(ORDER[last - 1], 0, 4, last - 1)
+            count(ORDER[last - 1], False, False)
+            count(j, False, True)
+            mask_difference(j, 2, 4)
+            row_sums(j, 0, 2, last)
             counts_sb = post.tile([P, B], F32, name="counts_sb", tag="counts_sb", bufs=1)
             nc.vector.tensor_copy(out=counts_sb[:], in_=counts[:])
             bk = bank_f32(next_bank(4))
@@ -487,7 +485,7 @@ def tile_multipleembedding_kernel(tc, x, drop_mask, W, b1, b2, gamma, beta, out_
             nc.vector.reciprocal(
                 out=inv_count[:].rearrange("p (a c) -> p a c", c=1), in_=bk[:].rearrange("p (a c) -> p a c", c=P)[:, :, 0:1]
             )
-            row_sums(last, 2, 4, last + 1)
+            row_sums(j, 2, 4, last + 1)
 
             totals = small.tile([P, B_TILES], F32, name="totals", tag="totals")
             nc.vector.tensor_reduce(out=totals[:], in_=loss_cols[:], axis=AXIS_X, op=ALU.add)

@@ -22,11 +22,12 @@ CHUNKS = N // CHUNK
 W2_CHUNK = 512
 W2_CHUNKS = N // W2_CHUNK
 RING = 6
+EARLY = 2
+M_SLOTS = 4
 ORDER = (6, 7, 0, 1, 2, 3, 4, 5)
 V_COLS_TAIL = 256
 V_COLS_WINDOW = 320
 V_COLS_LOOP = 0
-COUNT_BANK = 7
 LOSS_COLS = W2_CHUNKS + 1
 
 BF16 = mybir.dt.bfloat16
@@ -44,7 +45,7 @@ def tile_multipleembedding_kernel(tc, x, drop_mask, W, b1, b2, gamma, beta, out_
     with ExitStack() as ctx:
         const = ctx.enter_context(tc.tile_pool(name="const", bufs=1))
         keep = ctx.enter_context(tc.tile_pool(name="keep", bufs=1))
-        ring = ctx.enter_context(tc.tile_pool(name="ring", bufs=RING))
+        ring_early = ctx.enter_context(tc.tile_pool(name="ring_early", bufs=EARLY))
         psum = ctx.enter_context(tc.psum_pool(name="psum", bufs=1))
 
         def bank_f32(k):
@@ -61,8 +62,9 @@ def tile_multipleembedding_kernel(tc, x, drop_mask, W, b1, b2, gamma, beta, out_
         nc.vector.memset(spread[:], 0.0)
         neg_half = const.tile([P, 1], F32, name="neg_half")
         nc.vector.memset(neg_half[:], -0.5)
-        ones_b = const.tile([P, P], BF16, name="ones_b")
-        nc.vector.memset(ones_b[:], 1.0)
+        neg_ident_b = const.tile([P, P], BF16, name="neg_ident_b")
+        nc.vector.tensor_scalar_mul(out=neg_ident_b[:], in0=ident_b[:], scalar1=-1.0)
+        count_cols = const.tile([P, B_TILES, CHUNKS], F32, name="count_cols")
         rows_sb = const.tile([P, P], BF16, name="rows_sb")
         nc.vector.memset(rows_sb[:], 0.0)
         nc.scalar.dma_start(out=rows_sb[0:D_TILES, :], in_=b1.rearrange("(t p) -> t p", p=P))
@@ -71,7 +73,8 @@ def tile_multipleembedding_kernel(tc, x, drop_mask, W, b1, b2, gamma, beta, out_
         beta_b = const.tile([P, D], BF16, name="beta_b")
         bias_cols = const.tile([P, D_TILES + N_TILES], F32, name="bias_cols")
 
-        x_t = keep.tile([P, N_TILES, B], BF16, name="x_t")
+        x_nat = keep.tile([P, B_TILES, N], BF16, name="x_nat")
+        nz_t = keep.tile([P, N_TILES, B], BF16, name="nz_t")
         wt_codes = keep.tile([P, N_PASSES, D], U32, name="wt_codes", align_bytes=64)
         wt_scales = keep.tile([P, N_PASSES, D], U8, name="wt_scales", align_bytes=64)
         h_codes = keep.tile([P, N_PASSES, B], U32, name="h_codes", align_bytes=64)
@@ -100,11 +103,11 @@ def tile_multipleembedding_kernel(tc, x, drop_mask, W, b1, b2, gamma, beta, out_
             w_again[j] = again.tile([P, D_TILES, W2_CHUNK], BF16, name="w_again", tag="w_again")
             nc.sync.dma_start(out=w_again[j][:], in_=w_view[:, :, j * W2_CHUNK : (j + 1) * W2_CHUNK])
 
-        def regroup_w2(pool, w_rows, first, j, gd, v_cols):
+        def regroup_w2(ring, pool, tag, bufs, w_rows, first, j, gd, v_cols):
             if gd == 0:
                 w2_codes[j] = ring.tile([P, D_PASSES, W2_CHUNK], U32, name="w2c", tag="w2c", align_bytes=64)
                 w2_scales[j] = ring.tile([P, D_PASSES, W2_CHUNK], U8, name="w2s", tag="w2s", align_bytes=64)
-            grouped = pool.tile([P, W2_CHUNK, 4], BF16, name="w2g", tag="w2g", bufs=2, align_bytes=64)
+            grouped = pool.tile([P, W2_CHUNK, 4], BF16, name="w2g", tag=tag, bufs=bufs, align_bytes=64)
             for engine_copy, lo, hi in (
                 (nc.vector.tensor_copy, 0, v_cols),
                 (nc.scalar.copy, v_cols, W2_CHUNK),
@@ -131,7 +134,7 @@ def tile_multipleembedding_kernel(tc, x, drop_mask, W, b1, b2, gamma, beta, out_
         t_turn = [0]
 
         def next_t_bank():
-            t_turn[0] = (t_turn[0] + 1) % 3
+            t_turn[0] = (t_turn[0] + 1) % 4
             return 4 + t_turn[0]
 
 
@@ -148,24 +151,38 @@ def tile_multipleembedding_kernel(tc, x, drop_mask, W, b1, b2, gamma, beta, out_
             )
 
         with tc.tile_pool(name="stage", bufs=2) as stage:
-            x_in = {}
+            nz_in = {}
             m_in = {}
             w_in = {}
 
             def load(c):
                 cols = slice(c * CHUNK, (c + 1) * CHUNK)
-                x_in[c] = stage.tile([P, B_TILES, CHUNK], BF16, name="x_in", tag="x_in")
-                nc.sync.dma_start(out=x_in[c][:], in_=x_view[:, :, cols])
+                nc.sync.dma_start(out=x_nat[:, :, cols], in_=x_view[:, :, cols])
                 m_in[c] = stage.tile([P, B_TILES, CHUNK], BF16, name="m_in", tag="m_in")
                 nc.sync.dma_start(out=m_in[c][:], in_=m_view[:, :, cols])
                 w_in[c] = stage.tile([P, D_TILES, CHUNK], BF16, name="w_in", tag="w_in")
                 nc.sync.dma_start(out=w_in[c][:], in_=w_view[:, :, cols])
 
             def mask_x(c):
-                nc.vector.tensor_tensor(out=m_in[c][:], in0=x_in[c][:], in1=m_in[c][:], op=ALU.mult)
+                cols = slice(c * CHUNK, (c + 1) * CHUNK)
+                nc.vector.tensor_tensor(out=m_in[c][:], in0=x_nat[:, :, cols], in1=m_in[c][:], op=ALU.mult)
+
+            def mark_not_zero(c):
+                cols = slice(c * CHUNK, (c + 1) * CHUNK)
+                nz_in[c] = stage.tile([P, B_TILES, CHUNK], BF16, name="nz_in", tag="nz_in")
+                for bt in range(B_TILES):
+                    nc.vector.tensor_scalar(
+                        out=nz_in[c][:, bt, :],
+                        in0=x_nat[:, bt, cols],
+                        scalar1=0.0,
+                        scalar2=None,
+                        op0=ALU.not_equal,
+                        op1=ALU.add,
+                        accum_out=count_cols[:, bt, c : c + 1],
+                    )
 
             def transpose_x(c):
-                xc = x_in[c]
+                xc = nz_in[c]
                 for pair in range(CHUNK // (2 * P)):
                     bk = bank_bf16(next_bank(8))
                     for half in range(2):
@@ -175,7 +192,7 @@ def tile_multipleembedding_kernel(tc, x, drop_mask, W, b1, b2, gamma, beta, out_
                                 bk[:, B * half + P * bt : B * half + P * (bt + 1)], xc[:, bt, first : first + P], ident_b[:]
                             )
                     nt0 = (CHUNK // P) * c + 2 * pair
-                    dst = x_t[:, nt0 : nt0 + 2, :].rearrange("p a b -> p (a b)")
+                    dst = nz_t[:, nt0 : nt0 + 2, :].rearrange("p a b -> p (a b)")
                     if pair % 2 == 0:
                         nc.vector.tensor_copy(out=dst, in_=bk[:])
                     else:
@@ -183,11 +200,11 @@ def tile_multipleembedding_kernel(tc, x, drop_mask, W, b1, b2, gamma, beta, out_
                     drain(1)
 
             def scale_and_quantise_h(g, h_words):
-                grouped = stage.tile([P, 4 * B], BF16, name="hg", tag="hg", align_bytes=64)
-                nc.vector.tensor_scalar_mul(out=grouped[:], in0=h_words[:].bitcast(BF16), scalar1=KEEP_SCALE)
+                grouped = h_words[:].bitcast(BF16)
+                nc.vector.tensor_scalar_mul(out=grouped, in0=grouped, scalar1=KEEP_SCALE)
                 later(
                     lambda: nc.vector.quantize_mx(
-                        out=h_codes[:, g, :].bitcast(FP8X4), scales=h_scales[:, g, :], in_=grouped[:]
+                        out=h_codes[:, g, :].bitcast(FP8X4), scales=h_scales[:, g, :], in_=grouped
                     )
                 )
 
@@ -195,7 +212,7 @@ def tile_multipleembedding_kernel(tc, x, drop_mask, W, b1, b2, gamma, beta, out_
                 xm = m_in[c]
                 for gl in range(CHUNK // K_PASS):
                     g = c * (CHUNK // K_PASS) + gl
-                    h_words = stage.tile([P, 2 * B], F32, name="h_words", tag="h_words")
+                    h_words = stage.tile([P, 2 * B], F32, name="h_words", tag="h_words", bufs=3, align_bytes=64)
                     hw_view = h_words[:].rearrange("p (c u) -> p c u", u=2)
                     for pr in range(B_TILES // 2):
                         bk = bank_f32(next_bank(8))
@@ -243,11 +260,13 @@ def tile_multipleembedding_kernel(tc, x, drop_mask, W, b1, b2, gamma, beta, out_
 
             load(0)
             load(1)
+            mark_not_zero(0)
             mask_x(0)
             for c in range(CHUNKS):
                 transpose_x(c)
                 prepare_h(c)
                 if c + 1 < CHUNKS:
+                    mark_not_zero(c + 1)
                     mask_x(c + 1)
                 prepare_w_first(c, c == CHUNKS - 1)
                 if c + 2 < CHUNKS:
@@ -258,13 +277,13 @@ def tile_multipleembedding_kernel(tc, x, drop_mask, W, b1, b2, gamma, beta, out_
             drain(1)
             for j in ORDER[0:2]:
                 for gd in range(D_PASSES):
-                    regroup_w2(stage, w_in[CHUNKS - 1], W2_CHUNK * (j % 2), j, gd, V_COLS_TAIL)
+                    regroup_w2(ring_early, stage, "wtg", 3, w_in[CHUNKS - 1], W2_CHUNK * (j % 2), j, gd, V_COLS_TAIL)
                     drain(1)
             drain(0)
 
-        with tc.tile_pool(name="again", bufs=2) as again, tc.tile_pool(name="post", bufs=2) as post, tc.tile_pool(
-            name="small", bufs=2
-        ) as small:
+        with tc.tile_pool(name="ring_late", bufs=RING) as ring_late, tc.tile_pool(name="again", bufs=2) as again, tc.tile_pool(
+            name="post", bufs=2
+        ) as post, tc.tile_pool(name="small", bufs=2) as small:
             enc_t = post.tile([P, D_TILES, B], F32, name="enc_t", tag="enc_t", bufs=1)
             e_codes = post.tile([P, D_PASSES, B], U32, name="e_codes", tag="e_codes", bufs=1, align_bytes=64)
             e_scales = post.tile([P, D_PASSES, B], U8, name="e_scales", tag="e_scales", bufs=1, align_bytes=64)
@@ -293,7 +312,7 @@ def tile_multipleembedding_kernel(tc, x, drop_mask, W, b1, b2, gamma, beta, out_
 
             def ln_transpose(bt):
                 b_cols = slice(P * bt, P * (bt + 1))
-                enc = post.tile([P, D], F32, name="enc", tag="enc")
+                enc = ln_rows[:, bt % 2, :]
                 part_sum = small.tile([P, 2], F32, name="part_sum", tag="part_sum")
                 for dh in range(2):
                     bk = bank_f32(next_t_bank())
@@ -317,11 +336,9 @@ def tile_multipleembedding_kernel(tc, x, drop_mask, W, b1, b2, gamma, beta, out_
 
             def ln_square(bt):
                 t = ln[bt]
-                fin = post.tile([P, D], F32, name="fin", tag="fin")
+                fin = ln_rows[:, 2 + bt % 2, :]
                 sq_sum = small.tile([P, 1], F32, name="sq_sum", tag="sq_sum")
-                nc.scalar.activation(
-                    out=fin[:], in_=t["enc"][:], func=ACT.Square, bias=t["neg_mean"][:], accum_out=sq_sum[:]
-                )
+                nc.scalar.activation(out=fin, in_=t["enc"], func=ACT.Square, bias=t["neg_mean"][:], accum_out=sq_sum[:])
                 t["fin"] = fin
                 t["sq_sum"] = sq_sum
 
@@ -339,15 +356,12 @@ def tile_multipleembedding_kernel(tc, x, drop_mask, W, b1, b2, gamma, beta, out_
                 t = ln[bt]
                 fin = t["fin"]
                 nc.vector.scalar_tensor_tensor(
-                    out=fin[:], in0=t["enc"][:], scalar=t["neg_mean"][:], in1=gamma_b[:], op0=ALU.add, op1=ALU.mult
+                    out=fin, in0=t["enc"], scalar=t["neg_mean"][:], in1=gamma_b[:], op0=ALU.add, op1=ALU.mult
                 )
-                nc.vector.scalar_tensor_tensor(
-                    out=fin[:], in0=fin[:], scalar=t["rstd"][:], in1=beta_b[:], op0=ALU.mult, op1=ALU.add
-                )
-                nc.sync.dma_start(out=out_0[P * bt : P * (bt + 1), :], in_=fin[:])
+                nc.vector.scalar_tensor_tensor(out=fin, in0=fin, scalar=t["rstd"][:], in1=beta_b[:], op0=ALU.mult, op1=ALU.add)
+                nc.sync.dma_start(out=out_0[P * bt : P * (bt + 1), :], in_=fin)
 
-            squares = {}
-            not_zero = {}
+            masked = {}
 
             def difference(j, ntl):
                 nt = 4 * j + ntl
@@ -364,50 +378,38 @@ def tile_multipleembedding_kernel(tc, x, drop_mask, W, b1, b2, gamma, beta, out_
                         stop=(gd == D_PASSES - 1),
                     )
                 nc.vector.scalar_tensor_tensor(
-                    out=squares[j][:, ntl, :],
+                    out=masked[j][:, ntl, :],
                     in0=acc[:],
                     scalar=bias_cols[:, D_TILES + nt : D_TILES + nt + 1],
-                    in1=x_t[:, nt, :],
+                    in1=nz_t[:, nt, :],
                     op0=ALU.add,
-                    op1=ALU.subtract,
+                    op1=ALU.mult,
                 )
-
-            def mask_difference(j, lo, hi):
-                flat = squares[j][:, lo:hi, :].rearrange("p a b -> p (a b)")
-                x_flat = x_t[:, 4 * j + lo : 4 * j + hi, :].rearrange("p a b -> p (a b)")
-                nc.vector.scalar_tensor_tensor(out=flat, in0=x_flat, scalar=0.0, in1=flat, op0=ALU.not_equal, op1=ALU.mult)
 
             def row_sums(j, lo, hi, col):
                 for bt in range(B_TILES):
                     bk = bank_f32(next_t_bank())
+                    nc.tensor.matmul(
+                        out=bk[:, 0 : P * (hi - lo)],
+                        lhsT=neg_ident_b[:],
+                        rhs=x_nat[:, bt, W2_CHUNK * j + P * lo : W2_CHUNK * j + P * hi],
+                        start=True,
+                        stop=False,
+                    )
                     for ntl in range(lo, hi):
-                        nc.tensor.transpose(
-                            bk[:, P * (ntl - lo) : P * (ntl - lo + 1)], squares[j][:, ntl, P * bt : P * (bt + 1)], ident_f[:]
+                        nc.tensor.matmul(
+                            out=bk[:, P * (ntl - lo) : P * (ntl - lo + 1)],
+                            lhsT=masked[j][:, ntl, P * bt : P * (bt + 1)],
+                            rhs=ident_f[:],
+                            is_transpose=True,
+                            start=False,
+                            stop=(ntl == hi - 1),
                         )
                     nc.scalar.activation(
                         out=junk[:, 0 : P * (hi - lo)],
                         in_=bk[:, 0 : P * (hi - lo)],
                         func=ACT.Square,
                         accum_out=loss_cols[:, bt, col : col + 1],
-                    )
-
-            def mark_not_zero(j):
-                not_zero[j] = post.tile([P, 4, B], BF16, name="nz", tag="nz")
-                nc.vector.tensor_single_scalar(
-                    out=not_zero[j][:].rearrange("p a b -> p (a b)"),
-                    in_=x_t[:, 4 * j : 4 * j + 4, :].rearrange("p a b -> p (a b)"),
-                    scalar=0.0,
-                    op=ALU.not_equal,
-                )
-
-            def count(j, opening, closing):
-                for ntl in range(4):
-                    nc.tensor.matmul(
-                        out=counts[:],
-                        lhsT=ones_b[:],
-                        rhs=not_zero[j][:, ntl, :],
-                        start=(opening and ntl == 0),
-                        stop=(closing and ntl == 3),
                     )
 
             junk = post.tile([P, BANK_F32], BF16, name="junk", tag="junk", bufs=1)
@@ -420,7 +422,7 @@ def tile_multipleembedding_kernel(tc, x, drop_mask, W, b1, b2, gamma, beta, out_
             for d_tile in range(D_TILES):
                 j = d_tile // 2
                 gd = d_tile % 2
-                regroup_w2(again, w_again[j], 0, j, gd, V_COLS_WINDOW)
+                regroup_w2(ring_late, again, "w2g", 2, w_again[j], 0, j, gd, V_COLS_WINDOW)
                 drain(1)
                 if gd == 1 and j + 2 < RING:
                     reload(j + 2)
@@ -434,57 +436,45 @@ def tile_multipleembedding_kernel(tc, x, drop_mask, W, b1, b2, gamma, beta, out_
             drain(0)
             regroup_enc(1, B // 2)
             drain(0)
-            counts = bank_f32(COUNT_BANK)
+            m_ring = keep.tile([P, M_SLOTS, 4, B], F32, name="m_ring", tag="wt_codes", align_bytes=64)
+            ln_rows = keep.tile([P, 4, D], F32, name="ln_rows", tag="h_codes", align_bytes=64)
+            row_count = small.tile([P, B_TILES], F32, name="row_count", tag="row_count")
+            nc.vector.tensor_reduce(out=row_count[:], in_=count_cols[:], axis=AXIS_X, op=ALU.add)
+            inv_count = small.tile([P, B_TILES], F32, name="inv_count", tag="inv_count")
+            nc.vector.reciprocal(out=inv_count[:], in_=row_count[:])
             ln_transpose(0)
 
             last = W2_CHUNKS - 1
             for pos in range(last):
                 j = ORDER[pos]
-                squares[j] = post.tile([P, 4, B], F32, name="diff", tag="diff", bufs=3)
+                masked[j] = m_ring[:, pos % M_SLOTS, :, :]
                 for ntl in range(4):
                     difference(j, ntl)
                 if 1 <= pos <= B_TILES:
                     ln_rstd(pos - 1)
-                mask_difference(j, 0, 4)
                 if pos >= 1:
                     row_sums(ORDER[pos - 1], 0, 4, pos - 1)
-                    count(ORDER[pos - 1], pos == 1, False)
                 if 1 <= pos <= B_TILES:
                     ln_final(pos - 1)
                 if pos < B_TILES:
                     ln_mean(pos)
                     ln_square(pos)
-                mark_not_zero(j)
                 drain(0)
                 if pos + 1 < B_TILES:
                     ln_transpose(pos + 1)
                 if RING + pos < W2_CHUNKS:
                     coming = ORDER[RING + pos]
-                    regroup_w2(again, w_again[coming], 0, coming, 0, V_COLS_LOOP)
-                    regroup_w2(again, w_again[coming], 0, coming, 1, V_COLS_LOOP)
+                    regroup_w2(ring_late, again, "w2g", 2, w_again[coming], 0, coming, 0, V_COLS_LOOP)
+                    regroup_w2(ring_late, again, "w2g", 2, w_again[coming], 0, coming, 1, V_COLS_LOOP)
 
             j = ORDER[last]
-            squares[j] = post.tile([P, 4, B], F32, name="diff", tag="diff", bufs=3)
-            mark_not_zero(j)
+            masked[j] = m_ring[:, last % M_SLOTS, :, :]
             difference(j, 0)
             difference(j, 1)
-            mask_difference(j, 0, 2)
             difference(j, 2)
             difference(j, 3)
             row_sums(ORDER[last - 1], 0, 4, last - 1)
-            count(ORDER[last - 1], False, False)
-            count(j, False, True)
-            mask_difference(j, 2, 4)
             row_sums(j, 0, 2, last)
-            counts_sb = post.tile([P, B], F32, name="counts_sb", tag="counts_sb", bufs=1)
-            nc.vector.tensor_copy(out=counts_sb[:], in_=counts[:])
-            bk = bank_f32(next_bank(4))
-            for bt in range(B_TILES):
-                nc.tensor.transpose(bk[:, P * bt : P * (bt + 1)], counts_sb[:, P * bt : P * (bt + 1)], ident_f[:])
-            inv_count = small.tile([P, B_TILES], F32, name="inv_count", tag="inv_count")
-            nc.vector.reciprocal(
-                out=inv_count[:].rearrange("p (a c) -> p a c", c=1), in_=bk[:].rearrange("p (a c) -> p a c", c=P)[:, :, 0:1]
-            )
             row_sums(j, 2, 4, last + 1)
 
             totals = small.tile([P, B_TILES], F32, name="totals", tag="totals")

@@ -21,7 +21,7 @@ CHUNK = 1024
 CHUNKS = N // CHUNK
 W2_CHUNK = 512
 W2_CHUNKS = N // W2_CHUNK
-RING = 6
+LATE = 4
 EARLY = 2
 M_SLOTS = 4
 ORDER = (6, 7, 0, 1, 2, 3, 4, 5)
@@ -29,6 +29,8 @@ V_COLS_TAIL = 256
 V_COLS_WINDOW = 320
 V_COLS_LOOP = 0
 LOSS_COLS = W2_CHUNKS + 1
+COUNT_BANK = 7
+STAGE_BANKS = 7
 
 BF16 = mybir.dt.bfloat16
 F32 = mybir.dt.float32
@@ -46,6 +48,7 @@ def tile_multipleembedding_kernel(tc, x, drop_mask, W, b1, b2, gamma, beta, out_
         const = ctx.enter_context(tc.tile_pool(name="const", bufs=1))
         keep = ctx.enter_context(tc.tile_pool(name="keep", bufs=1))
         ring_early = ctx.enter_context(tc.tile_pool(name="ring_early", bufs=EARLY))
+        w_pool = ctx.enter_context(tc.tile_pool(name="w_pool", bufs=2))
         psum = ctx.enter_context(tc.psum_pool(name="psum", bufs=1))
 
         def bank_f32(k):
@@ -64,7 +67,10 @@ def tile_multipleembedding_kernel(tc, x, drop_mask, W, b1, b2, gamma, beta, out_
         nc.vector.memset(neg_half[:], -0.5)
         neg_ident_b = const.tile([P, P], BF16, name="neg_ident_b")
         nc.vector.tensor_scalar_mul(out=neg_ident_b[:], in0=ident_b[:], scalar1=-1.0)
-        count_cols = const.tile([P, B_TILES, CHUNKS], F32, name="count_cols")
+        ones_b = const.tile([P, 2], BF16, name="ones_b")
+        nc.vector.memset(ones_b[:], 1.0)
+        zeros_b = const.tile([P, 2 * B_TILES], BF16, name="zeros_b")
+        nc.vector.memset(zeros_b[:], 0.0)
         rows_sb = const.tile([P, P], BF16, name="rows_sb")
         nc.vector.memset(rows_sb[:], 0.0)
         nc.scalar.dma_start(out=rows_sb[0:D_TILES, :], in_=b1.rearrange("(t p) -> t p", p=P))
@@ -99,9 +105,9 @@ def tile_multipleembedding_kernel(tc, x, drop_mask, W, b1, b2, gamma, beta, out_
                 waiting[emitted[0]]()
                 emitted[0] += 1
 
-        def reload(j):
-            w_again[j] = again.tile([P, D_TILES, W2_CHUNK], BF16, name="w_again", tag="w_again")
-            nc.sync.dma_start(out=w_again[j][:], in_=w_view[:, :, j * W2_CHUNK : (j + 1) * W2_CHUNK])
+        def reload(c):
+            w_again[c] = w_pool.tile([P, D_TILES, CHUNK], BF16, name="w_again", tag="w_in")
+            nc.sync.dma_start(out=w_again[c][:], in_=w_view[:, :, c * CHUNK : (c + 1) * CHUNK])
 
         def regroup_w2(ring, pool, tag, bufs, w_rows, first, j, gd, v_cols):
             if gd == 0:
@@ -151,7 +157,6 @@ def tile_multipleembedding_kernel(tc, x, drop_mask, W, b1, b2, gamma, beta, out_
             )
 
         with tc.tile_pool(name="stage", bufs=2) as stage:
-            nz_in = {}
             m_in = {}
             w_in = {}
 
@@ -160,43 +165,36 @@ def tile_multipleembedding_kernel(tc, x, drop_mask, W, b1, b2, gamma, beta, out_
                 nc.sync.dma_start(out=x_nat[:, :, cols], in_=x_view[:, :, cols])
                 m_in[c] = stage.tile([P, B_TILES, CHUNK], BF16, name="m_in", tag="m_in")
                 nc.sync.dma_start(out=m_in[c][:], in_=m_view[:, :, cols])
-                w_in[c] = stage.tile([P, D_TILES, CHUNK], BF16, name="w_in", tag="w_in")
+                w_in[c] = w_pool.tile([P, D_TILES, CHUNK], BF16, name="w_in", tag="w_in")
                 nc.sync.dma_start(out=w_in[c][:], in_=w_view[:, :, cols])
 
             def mask_x(c):
                 cols = slice(c * CHUNK, (c + 1) * CHUNK)
                 nc.vector.tensor_tensor(out=m_in[c][:], in0=x_nat[:, :, cols], in1=m_in[c][:], op=ALU.mult)
 
-            def mark_not_zero(c):
-                cols = slice(c * CHUNK, (c + 1) * CHUNK)
-                nz_in[c] = stage.tile([P, B_TILES, CHUNK], BF16, name="nz_in", tag="nz_in")
+            def count(nt):
                 for bt in range(B_TILES):
-                    nc.vector.tensor_scalar(
-                        out=nz_in[c][:, bt, :],
-                        in0=x_nat[:, bt, cols],
-                        scalar1=0.0,
-                        scalar2=None,
-                        op0=ALU.not_equal,
-                        op1=ALU.add,
-                        accum_out=count_cols[:, bt, c : c + 1],
+                    nc.tensor.matmul(
+                        out=counts[:, 2 * bt : 2 * bt + 2],
+                        lhsT=nz_t[:, nt, P * bt : P * (bt + 1)],
+                        rhs=ones_b[:],
+                        start=False,
+                        stop=False,
                     )
 
             def transpose_x(c):
-                xc = nz_in[c]
+                xc = x_nat
                 for pair in range(CHUNK // (2 * P)):
-                    bk = bank_bf16(next_bank(8))
+                    bk = bank_bf16(next_bank(STAGE_BANKS))
                     for half in range(2):
-                        first = P * (2 * pair + half)
+                        first = CHUNK * c + P * (2 * pair + half)
                         for bt in range(B_TILES):
                             nc.tensor.transpose(
                                 bk[:, B * half + P * bt : B * half + P * (bt + 1)], xc[:, bt, first : first + P], ident_b[:]
                             )
                     nt0 = (CHUNK // P) * c + 2 * pair
                     dst = nz_t[:, nt0 : nt0 + 2, :].rearrange("p a b -> p (a b)")
-                    if pair % 2 == 0:
-                        nc.vector.tensor_copy(out=dst, in_=bk[:])
-                    else:
-                        nc.scalar.copy(out=dst, in_=bk[:])
+                    nc.vector.tensor_single_scalar(out=dst, in_=bk[:], scalar=0.0, op=ALU.not_equal)
                     drain(1)
 
             def scale_and_quantise_h(g, h_words):
@@ -215,7 +213,7 @@ def tile_multipleembedding_kernel(tc, x, drop_mask, W, b1, b2, gamma, beta, out_
                     h_words = stage.tile([P, 2 * B], F32, name="h_words", tag="h_words", bufs=3, align_bytes=64)
                     hw_view = h_words[:].rearrange("p (c u) -> p c u", u=2)
                     for pr in range(B_TILES // 2):
-                        bk = bank_f32(next_bank(8))
+                        bk = bank_f32(next_bank(STAGE_BANKS))
                         planes = bk[:].rearrange("p (u c) -> p u c", u=2)
                         for bl in range(2):
                             words = xm[:, 2 * pr + bl, :].bitcast(F32)
@@ -242,7 +240,7 @@ def tile_multipleembedding_kernel(tc, x, drop_mask, W, b1, b2, gamma, beta, out_
                         grouped = stage.tile([P, 4 * BANK_F32], BF16, name="wtg", tag="wtg", bufs=3, align_bytes=64)
                         g_words = grouped[:].bitcast(F32).rearrange("p (c u) -> p c u", u=2)
                         for j in range(2):
-                            bk = bank_f32(next_bank(8))
+                            bk = bank_f32(next_bank(STAGE_BANKS))
                             planes = bk[:].rearrange("p (u c) -> p u c", u=2)
                             for dd in range(2):
                                 words = wn[:, 4 * half + 2 * j + dd, :].bitcast(F32)
@@ -260,18 +258,28 @@ def tile_multipleembedding_kernel(tc, x, drop_mask, W, b1, b2, gamma, beta, out_
 
             load(0)
             load(1)
-            mark_not_zero(0)
             mask_x(0)
+            counts = bank_f32(COUNT_BANK)
+            nc.tensor.matmul(out=counts[:, 0 : 2 * B_TILES], lhsT=ident_b[:], rhs=zeros_b[:], start=True, stop=False)
             for c in range(CHUNKS):
                 transpose_x(c)
                 prepare_h(c)
                 if c + 1 < CHUNKS:
-                    mark_not_zero(c + 1)
                     mask_x(c + 1)
                 prepare_w_first(c, c == CHUNKS - 1)
+                for nt in range((CHUNK // P) * c, (CHUNK // P) * (c + 1)):
+                    count(nt)
                 if c + 2 < CHUNKS:
                     load(c + 2)
-            bk = bank_bf16(next_bank(8))
+                elif c + 2 == CHUNKS:
+                    reload(0)
+            nc.tensor.matmul(out=counts[:, 0 : 2 * B_TILES], lhsT=ident_b[:], rhs=zeros_b[:], start=False, stop=True)
+            inv_count = const.tile([P, B_TILES], F32, name="inv_count")
+            nc.vector.reciprocal(
+                out=inv_count[:].rearrange("p (a c) -> p a c", c=1),
+                in_=counts[:, 0 : 2 * B_TILES].rearrange("p (a c) -> p a c", c=2)[:, :, 0:1],
+            )
+            bk = bank_bf16(next_bank(STAGE_BANKS))
             nc.tensor.transpose(bk[:, 0:P], rows_sb[:], ident_b[:])
             nc.vector.tensor_copy(out=bias_cols[:], in_=bk[:, 0 : D_TILES + N_TILES])
             drain(1)
@@ -280,8 +288,9 @@ def tile_multipleembedding_kernel(tc, x, drop_mask, W, b1, b2, gamma, beta, out_
                     regroup_w2(ring_early, stage, "wtg", 3, w_in[CHUNKS - 1], W2_CHUNK * (j % 2), j, gd, V_COLS_TAIL)
                     drain(1)
             drain(0)
+            reload(1)
 
-        with tc.tile_pool(name="ring_late", bufs=RING) as ring_late, tc.tile_pool(name="again", bufs=2) as again, tc.tile_pool(
+        with tc.tile_pool(name="ring_late", bufs=LATE) as ring_late, tc.tile_pool(name="again", bufs=2) as again, tc.tile_pool(
             name="post", bufs=2
         ) as post, tc.tile_pool(name="small", bufs=2) as small:
             enc_t = post.tile([P, D_TILES, B], F32, name="enc_t", tag="enc_t", bufs=1)
@@ -415,17 +424,15 @@ def tile_multipleembedding_kernel(tc, x, drop_mask, W, b1, b2, gamma, beta, out_
             junk = post.tile([P, BANK_F32], BF16, name="junk", tag="junk", bufs=1)
             loss_cols = post.tile([P, B_TILES, LOSS_COLS], F32, name="loss_cols", tag="loss_cols", bufs=1)
 
-            reload(0)
-            reload(1)
             nc.sync.dma_start(out=gamma_b[:], in_=gamma.partition_broadcast(P))
             nc.sync.dma_start(out=beta_b[:], in_=beta.partition_broadcast(P))
             for d_tile in range(D_TILES):
                 j = d_tile // 2
                 gd = d_tile % 2
-                regroup_w2(ring_late, again, "w2g", 2, w_again[j], 0, j, gd, V_COLS_WINDOW)
+                regroup_w2(ring_late, again, "w2g", 2, w_again[j // 2], W2_CHUNK * (j % 2), j, gd, V_COLS_WINDOW)
                 drain(1)
-                if gd == 1 and j + 2 < RING:
-                    reload(j + 2)
+                if d_tile == 3:
+                    reload(2)
                 acc = bank_f32(d_tile % 4)
                 for g in range(N_PASSES):
                     first_matmul(acc, d_tile, g)
@@ -438,10 +445,6 @@ def tile_multipleembedding_kernel(tc, x, drop_mask, W, b1, b2, gamma, beta, out_
             drain(0)
             m_ring = keep.tile([P, M_SLOTS, 4, B], F32, name="m_ring", tag="wt_codes", align_bytes=64)
             ln_rows = keep.tile([P, 4, D], F32, name="ln_rows", tag="h_codes", align_bytes=64)
-            row_count = small.tile([P, B_TILES], F32, name="row_count", tag="row_count")
-            nc.vector.tensor_reduce(out=row_count[:], in_=count_cols[:], axis=AXIS_X, op=ALU.add)
-            inv_count = small.tile([P, B_TILES], F32, name="inv_count", tag="inv_count")
-            nc.vector.reciprocal(out=inv_count[:], in_=row_count[:])
             ln_transpose(0)
 
             last = W2_CHUNKS - 1
@@ -462,10 +465,12 @@ def tile_multipleembedding_kernel(tc, x, drop_mask, W, b1, b2, gamma, beta, out_
                 drain(0)
                 if pos + 1 < B_TILES:
                     ln_transpose(pos + 1)
-                if RING + pos < W2_CHUNKS:
-                    coming = ORDER[RING + pos]
-                    regroup_w2(ring_late, again, "w2g", 2, w_again[coming], 0, coming, 0, V_COLS_LOOP)
-                    regroup_w2(ring_late, again, "w2g", 2, w_again[coming], 0, coming, 1, V_COLS_LOOP)
+                if EARLY + LATE + pos < W2_CHUNKS:
+                    coming = ORDER[EARLY + LATE + pos]
+                    for gd in range(D_PASSES):
+                        regroup_w2(
+                            ring_early, again, "w2g", 2, w_again[coming // 2], W2_CHUNK * (coming % 2), coming, gd, V_COLS_LOOP
+                        )
 
             j = ORDER[last]
             masked[j] = m_ring[:, last % M_SLOTS, :, :]

@@ -160,17 +160,26 @@ def tile_multipleembedding_kernel(tc, x, drop_mask, W, b1, b2, gamma, beta, out_
             m_in = {}
             w_in = {}
 
+            def pieces_of(c):
+                return 2 if c == 0 else 1
+
             def load(c):
-                cols = slice(c * CHUNK, (c + 1) * CHUNK)
-                nc.sync.dma_start(out=x_nat[:, :, cols], in_=x_view[:, :, cols])
                 m_in[c] = stage.tile([P, B_TILES, CHUNK], BF16, name="m_in", tag="m_in")
-                nc.sync.dma_start(out=m_in[c][:], in_=m_view[:, :, cols])
                 w_in[c] = w_pool.tile([P, D_TILES, CHUNK], BF16, name="w_in", tag="w_in")
-                nc.sync.dma_start(out=w_in[c][:], in_=w_view[:, :, cols])
+                width = CHUNK // pieces_of(c)
+                for piece in range(pieces_of(c)):
+                    here = slice(piece * width, (piece + 1) * width)
+                    cols = slice(c * CHUNK + piece * width, c * CHUNK + (piece + 1) * width)
+                    nc.sync.dma_start(out=x_nat[:, :, cols], in_=x_view[:, :, cols])
+                    nc.sync.dma_start(out=m_in[c][:, :, here], in_=m_view[:, :, cols])
+                    nc.sync.dma_start(out=w_in[c][:, :, here], in_=w_view[:, :, cols])
 
             def mask_x(c):
-                cols = slice(c * CHUNK, (c + 1) * CHUNK)
-                nc.vector.tensor_tensor(out=m_in[c][:], in0=x_nat[:, :, cols], in1=m_in[c][:], op=ALU.mult)
+                width = CHUNK // pieces_of(c)
+                for piece in range(pieces_of(c)):
+                    here = slice(piece * width, (piece + 1) * width)
+                    cols = slice(c * CHUNK + piece * width, c * CHUNK + (piece + 1) * width)
+                    nc.vector.tensor_tensor(out=m_in[c][:, :, here], in0=x_nat[:, :, cols], in1=m_in[c][:, :, here], op=ALU.mult)
 
             def count(nt):
                 for bt in range(B_TILES):
@@ -197,21 +206,23 @@ def tile_multipleembedding_kernel(tc, x, drop_mask, W, b1, b2, gamma, beta, out_
                     nc.vector.tensor_single_scalar(out=dst, in_=bk[:], scalar=0.0, op=ALU.not_equal)
                     drain(1)
 
-            def scale_and_quantise_h(g, h_words):
-                grouped = h_words[:].bitcast(BF16)
+            def scale_and_quantise_h(c, h_words):
+                passes = slice((CHUNK // K_PASS) * c, (CHUNK // K_PASS) * (c + 1))
+                grouped = h_words[:].rearrange("p g w -> p (g w)").bitcast(BF16)
                 nc.vector.tensor_scalar_mul(out=grouped, in0=grouped, scalar1=KEEP_SCALE)
                 later(
                     lambda: nc.vector.quantize_mx(
-                        out=h_codes[:, g, :].bitcast(FP8X4), scales=h_scales[:, g, :], in_=grouped
+                        out=h_codes[:, passes, :].rearrange("p g b -> p (g b)").bitcast(FP8X4),
+                        scales=h_scales[:, passes, :].rearrange("p g b -> p (g b)"),
+                        in_=grouped,
                     )
                 )
 
             def prepare_h(c):
                 xm = m_in[c]
+                h_words = stage.tile([P, CHUNK // K_PASS, 2 * B], F32, name="h_words", tag="h_words", align_bytes=64)
                 for gl in range(CHUNK // K_PASS):
-                    g = c * (CHUNK // K_PASS) + gl
-                    h_words = stage.tile([P, 2 * B], F32, name="h_words", tag="h_words", bufs=3, align_bytes=64)
-                    hw_view = h_words[:].rearrange("p (c u) -> p c u", u=2)
+                    hw_view = h_words[:, gl, :].rearrange("p (c u) -> p c u", u=2)
                     for pr in range(B_TILES // 2):
                         bk = bank_f32(next_bank(STAGE_BANKS))
                         planes = bk[:].rearrange("p (u c) -> p u c", u=2)
@@ -225,36 +236,34 @@ def tile_multipleembedding_kernel(tc, x, drop_mask, W, b1, b2, gamma, beta, out_
                         nc.scalar.copy(
                             out=hw_view[:, 256 * pr : 256 * (pr + 1), :], in_=bk[:].rearrange("p (u c) -> p c u", u=2)
                         )
-                    drain(1)
-                    later(lambda g=g, h_words=h_words: scale_and_quantise_h(g, h_words))
+                drain(1)
+                later(lambda: scale_and_quantise_h(c, h_words))
 
-            def quantise_wt(g, half, grouped):
-                cols = slice(BANK_F32 * half, BANK_F32 * (half + 1))
-                nc.vector.quantize_mx(out=wt_codes[:, g, cols].bitcast(FP8X4), scales=wt_scales[:, g, cols], in_=grouped[:])
+            def quantise_wt(g, grouped):
+                nc.vector.quantize_mx(out=wt_codes[:, g, :].bitcast(FP8X4), scales=wt_scales[:, g, :], in_=grouped[:])
 
             def prepare_w_first(c, share):
                 wn = w_in[c]
                 for gl in range(CHUNK // K_PASS):
                     g = c * (CHUNK // K_PASS) + gl
-                    for half in range(2):
-                        grouped = stage.tile([P, 4 * BANK_F32], BF16, name="wtg", tag="wtg", bufs=3, align_bytes=64)
-                        g_words = grouped[:].bitcast(F32).rearrange("p (c u) -> p c u", u=2)
-                        for j in range(2):
-                            bk = bank_f32(next_bank(STAGE_BANKS))
-                            planes = bk[:].rearrange("p (u c) -> p u c", u=2)
-                            for dd in range(2):
-                                words = wn[:, 4 * half + 2 * j + dd, :].bitcast(F32)
-                                for u in range(2):
-                                    first = 256 * gl + P * u
-                                    nc.tensor.transpose(
-                                        planes[:, u, P * dd : P * (dd + 1)], words[:, first : first + P], ident_f[:]
-                                    )
-                            engine_copy = nc.vector.tensor_copy if (share and j == 1) else nc.scalar.copy
-                            engine_copy(
-                                out=g_words[:, 256 * j : 256 * (j + 1), :], in_=bk[:].rearrange("p (u c) -> p c u", u=2)
-                            )
-                        drain(1)
-                        later(lambda g=g, half=half, grouped=grouped: quantise_wt(g, half, grouped))
+                    grouped = stage.tile([P, 4 * D], BF16, name="wtg", tag="wtg", bufs=2, align_bytes=64)
+                    g_words = grouped[:].bitcast(F32).rearrange("p (c u) -> p c u", u=2)
+                    for j in range(D_TILES // 2):
+                        bk = bank_f32(next_bank(STAGE_BANKS))
+                        planes = bk[:].rearrange("p (u c) -> p u c", u=2)
+                        for dd in range(2):
+                            words = wn[:, 2 * j + dd, :].bitcast(F32)
+                            for u in range(2):
+                                first = 256 * gl + P * u
+                                nc.tensor.transpose(
+                                    planes[:, u, P * dd : P * (dd + 1)], words[:, first : first + P], ident_f[:]
+                                )
+                        engine_copy = nc.vector.tensor_copy if (share and j % 2 == 1) else nc.scalar.copy
+                        engine_copy(
+                            out=g_words[:, 256 * j : 256 * (j + 1), :], in_=bk[:].rearrange("p (u c) -> p c u", u=2)
+                        )
+                    drain(1)
+                    later(lambda g=g, grouped=grouped: quantise_wt(g, grouped))
 
             load(0)
             load(1)
@@ -266,7 +275,7 @@ def tile_multipleembedding_kernel(tc, x, drop_mask, W, b1, b2, gamma, beta, out_
                 prepare_h(c)
                 if c + 1 < CHUNKS:
                     mask_x(c + 1)
-                prepare_w_first(c, c == CHUNKS - 1)
+                prepare_w_first(c, False)
                 for nt in range((CHUNK // P) * c, (CHUNK // P) * (c + 1)):
                     count(nt)
                 if c + 2 < CHUNKS:
@@ -285,7 +294,7 @@ def tile_multipleembedding_kernel(tc, x, drop_mask, W, b1, b2, gamma, beta, out_
             drain(1)
             for j in ORDER[0:2]:
                 for gd in range(D_PASSES):
-                    regroup_w2(ring_early, stage, "wtg", 3, w_in[CHUNKS - 1], W2_CHUNK * (j % 2), j, gd, V_COLS_TAIL)
+                    regroup_w2(ring_early, stage, "wtg", 2, w_in[CHUNKS - 1], W2_CHUNK * (j % 2), j, gd, V_COLS_TAIL)
                     drain(1)
             drain(0)
             reload(1)

@@ -282,6 +282,8 @@ def tile_multipleembedding_kernel(tc, x, drop_mask, W, b1, b2, gamma, beta, out_
                     load(c + 2)
                 elif c + 2 == CHUNKS:
                     reload(0)
+                    nc.sync.dma_start(out=gamma_b[:], in_=gamma.partition_broadcast(P))
+                    nc.sync.dma_start(out=beta_b[:], in_=beta.partition_broadcast(P))
             nc.tensor.matmul(out=counts[:, 0 : 2 * B_TILES], lhsT=ident_b[:], rhs=zeros_b[:], start=False, stop=True)
             inv_count = const.tile([P, B_TILES], F32, name="inv_count")
             nc.vector.reciprocal(
@@ -433,8 +435,6 @@ def tile_multipleembedding_kernel(tc, x, drop_mask, W, b1, b2, gamma, beta, out_
             junk = post.tile([P, BANK_F32], BF16, name="junk", tag="junk", bufs=1)
             loss_cols = post.tile([P, B_TILES, LOSS_COLS], F32, name="loss_cols", tag="loss_cols", bufs=1)
 
-            nc.sync.dma_start(out=gamma_b[:], in_=gamma.partition_broadcast(P))
-            nc.sync.dma_start(out=beta_b[:], in_=beta.partition_broadcast(P))
             for d_tile in range(D_TILES):
                 j = d_tile // 2
                 gd = d_tile % 2

from contextlib import ExitStack

import concourse.mybir as mybir
from concourse.masks import make_identity

B, N, D = 512, 4096, 1024
FLOPS = 2 * 2 * B * N * D
KEEP_SCALE = 1.0 / 0.75
LN_EPS = 1e-5

P = 128
K_PASS = 512
BANK_F32 = 512
BANK_BF16 = 1024
B_TILES = B // P
D_TILES = D // P
N_TILES = N // P
N_PASSES = N // K_PASS
D_PASSES = D // K_PASS
CHUNK = 1024
CHUNKS = N // CHUNK
W2_CHUNK = 512
W2_CHUNKS = N // W2_CHUNK
LATE = 4
EARLY = 2
M_SLOTS = 4
ORDER = (6, 7, 0, 1, 2, 3, 4, 5)
V_COLS_TAIL = 256
V_COLS_WINDOW = 320
V_COLS_LOOP = 0
LOSS_COLS = W2_CHUNKS + 1
COUNT_BANK = 7
STAGE_BANKS = 7

BF16 = mybir.dt.bfloat16
F32 = mybir.dt.float32
U32 = mybir.dt.uint32
U8 = mybir.dt.uint8
FP8X4 = mybir.dt.float8_e4m3fn_x4
ALU = mybir.AluOpType
ACT = mybir.ActivationFunctionType
AXIS_X = mybir.AxisListType.X


def tile_multipleembedding_kernel(tc, x, drop_mask, W, b1, b2, gamma, beta, out_0, out_1):
    nc = tc.nc
    with ExitStack() as ctx:
        const = ctx.enter_context(tc.tile_pool(name="const", bufs=1))
        keep = ctx.enter_context(tc.tile_pool(name="keep", bufs=1))
        ring_early = ctx.enter_context(tc.tile_pool(name="ring_early", bufs=EARLY))
        w_pool = ctx.enter_context(tc.tile_pool(name="w_pool", bufs=2))
        psum = ctx.enter_context(tc.psum_pool(name="psum", bufs=1))

        def bank_f32(k):
            return psum.tile([P, BANK_F32], F32, name="bank%d" % k, tag="bank%d" % k)

        def bank_bf16(k):
            return psum.tile([P, BANK_BF16], BF16, name="bank%d" % k, tag="bank%d" % k)

        ident_f = const.tile([P, P], F32, name="ident_f")
        make_identity(nc, ident_f[:])
        ident_b = const.tile([P, P], BF16, name="ident_b")
        make_identity(nc, ident_b[:])
        spread = const.tile([P, P], F32, name="spread")
        nc.vector.memset(spread[:], 0.0)
        neg_half = const.tile([P, 1], F32, name="neg_half")
        nc.vector.memset(neg_half[:], -0.5)
        neg_ident_b = const.tile([P, P], BF16, name="neg_ident_b")
        nc.vector.tensor_scalar_mul(out=neg_ident_b[:], in0=ident_b[:], scalar1=-1.0)
        ones_b = const.tile([P, 2], BF16, name="ones_b")
        nc.vector.memset(ones_b[:], 1.0)
        zeros_b = const.tile([P, 2 * B_TILES], BF16, name="zeros_b")
        nc.vector.memset(zeros_b[:], 0.0)
        rows_sb = const.tile([P, P], BF16, name="rows_sb")
        nc.vector.memset(rows_sb[:], 0.0)
        nc.scalar.dma_start(out=rows_sb[0:D_TILES, :], in_=b1.rearrange("(t p) -> t p", p=P))
        nc.scalar.dma_start(out=rows_sb[D_TILES : D_TILES + N_TILES, :], in_=b2.rearrange("(t p) -> t p", p=P))
        gamma_b = const.tile([P, D], BF16, name="gamma_b")
        beta_b = const.tile([P, D], BF16, name="beta_b")
        bias_cols = const.tile([P, D_TILES + N_TILES], F32, name="bias_cols")

        x_nat = keep.tile([P, B_TILES, N], BF16, name="x_nat")
        nz_t = keep.tile([P, N_TILES, B], BF16, name="nz_t")
        wt_codes = keep.tile([P, N_PASSES, D], U32, name="wt_codes", align_bytes=64)
        wt_scales = keep.tile([P, N_PASSES, D], U8, name="wt_scales", align_bytes=64)
        h_codes = keep.tile([P, N_PASSES, B], U32, name="h_codes", align_bytes=64)
        h_scales = keep.tile([P, N_PASSES, B], U8, name="h_scales", align_bytes=64)

        x_view = x.rearrange("(t p) n -> p t n", p=P)
        m_view = drop_mask.rearrange("(t p) n -> p t n", p=P)
        w_view = W.rearrange("(t p) n -> p t n", p=P)

        w2_codes = {}
        w2_scales = {}

        w_again = {}
        waiting = []
        emitted = [0]

        def later(call):
            waiting.append(call)

        def drain(keep_back):
            while len(waiting) - emitted[0] > keep_back:
                waiting[emitted[0]]()
                emitted[0] += 1

        def reload(c):
            w_again[c] = w_pool.tile([P, D_TILES, CHUNK], BF16, name="w_again", tag="w_in")
            nc.sync.dma_start(out=w_again[c][:], in_=w_view[:, :, c * CHUNK : (c + 1) * CHUNK])

        def regroup_w2(ring, pool, tag, bufs, w_rows, first, j, gd, v_cols):
            if gd == 0:
                w2_codes[j] = ring.tile([P, D_PASSES, W2_CHUNK], U32, name="w2c", tag="w2c", align_bytes=64)
                w2_scales[j] = ring.tile([P, D_PASSES, W2_CHUNK], U8, name="w2s", tag="w2s", align_bytes=64)
            grouped = pool.tile([P, W2_CHUNK, 4], BF16, name="w2g", tag=tag, bufs=bufs, align_bytes=64)
            for engine_copy, lo, hi in (
                (nc.vector.tensor_copy, 0, v_cols),
                (nc.scalar.copy, v_cols, W2_CHUNK),
            ):
                if hi > lo:
                    engine_copy(
                        out=grouped[:, lo:hi, :].rearrange("p (c i) t -> p c t i", i=4),
                        in_=w_rows[:, 4 * gd : 4 * gd + 4, first + lo : first + hi].rearrange("p t (c i) -> p c t i", i=4),
                    )
            later(
                lambda: nc.vector.quantize_mx(
                    out=w2_codes[j][:, gd, :].bitcast(FP8X4),
                    scales=w2_scales[j][:, gd, :],
                    in_=grouped[:].rearrange("p c t -> p (c t)"),
                )
            )

        turn = [0]

        def next_bank(count):
            turn[0] = (turn[0] + 1) % count
            return turn[0]

        t_turn = [0]

        def next_t_bank():
            t_turn[0] = (t_turn[0] + 1) % 4
            return 4 + t_turn[0]


        def first_matmul(acc, d_tile, g):
            d_cols = slice(P * d_tile, P * (d_tile + 1))
            nc.tensor.matmul_mx(
                out=acc[:],
                lhsT=wt_codes[:, g, d_cols].bitcast(FP8X4),
                lhsT_scale=wt_scales[:, g, d_cols],
                rhs=h_codes[:, g, :].bitcast(FP8X4),
                rhs_scale=h_scales[:, g, :],
                start=(g == 0),
                stop=(g == N_PASSES - 1),
            )

        with tc.tile_pool(name="stage", bufs=2) as stage:
            m_in = {}
            w_in = {}

            def pieces_of(c):
                return 2 if c == 0 else 1

            def load(c):
                m_in[c] = stage.tile([P, B_TILES, CHUNK], BF16, name="m_in", tag="m_in")
                w_in[c] = w_pool.tile([P, D_TILES, CHUNK], BF16, name="w_in", tag="w_in")
                width = CHUNK // pieces_of(c)
                for piece in range(pieces_of(c)):
                    here = slice(piece * width, (piece + 1) * width)
                    cols = slice(c * CHUNK + piece * width, c * CHUNK + (piece + 1) * width)
                    nc.sync.dma_start(out=x_nat[:, :, cols], in_=x_view[:, :, cols])
                    nc.sync.dma_start(out=m_in[c][:, :, here], in_=m_view[:, :, cols])
                    nc.sync.dma_start(out=w_in[c][:, :, here], in_=w_view[:, :, cols])

            def mask_x(c):
                width = CHUNK // pieces_of(c)
                for piece in range(pieces_of(c)):
                    here = slice(piece * width, (piece + 1) * width)
                    cols = slice(c * CHUNK + piece * width, c * CHUNK + (piece + 1) * width)
                    nc.vector.tensor_tensor(out=m_in[c][:, :, here], in0=x_nat[:, :, cols], in1=m_in[c][:, :, here], op=ALU.mult)

            def count(nt):
                for bt in range(B_TILES):
                    nc.tensor.matmul(
                        out=counts[:, 2 * bt : 2 * bt + 2],
                        lhsT=nz_t[:, nt, P * bt : P * (bt + 1)],
                        rhs=ones_b[:],
                        start=False,
                        stop=False,
                    )

            def transpose_x(c):
                xc = x_nat
                for pair in range(CHUNK // (2 * P)):
                    bk = bank_bf16(next_bank(STAGE_BANKS))
                    for half in range(2):
                        first = CHUNK * c + P * (2 * pair + half)
                        for bt in range(B_TILES):
                            nc.tensor.transpose(
                                bk[:, B * half + P * bt : B * half + P * (bt + 1)], xc[:, bt, first : first + P], ident_b[:]
                            )
                    nt0 = (CHUNK // P) * c + 2 * pair
                    dst = nz_t[:, nt0 : nt0 + 2, :].rearrange("p a b -> p (a b)")
                    nc.vector.tensor_single_scalar(out=dst, in_=bk[:], scalar=0.0, op=ALU.not_equal)
                    drain(1)

            def scale_and_quantise_h(c, h_words):
                passes = slice((CHUNK // K_PASS) * c, (CHUNK // K_PASS) * (c + 1))
                grouped = h_words[:].rearrange("p g w -> p (g w)").bitcast(BF16)
                nc.vector.tensor_scalar_mul(out=grouped, in0=grouped, scalar1=KEEP_SCALE)
                later(
                    lambda: nc.vector.quantize_mx(
                        out=h_codes[:, passes, :].rearrange("p g b -> p (g b)").bitcast(FP8X4),
                        scales=h_scales[:, passes, :].rearrange("p g b -> p (g b)"),
                        in_=grouped,
                    )
                )

            def prepare_h(c):
                xm = m_in[c]
                h_words = stage.tile([P, CHUNK // K_PASS, 2 * B], F32, name="h_words", tag="h_words", align_bytes=64)
                for gl in range(CHUNK // K_PASS):
                    hw_view = h_words[:, gl, :].rearrange("p (c u) -> p c u", u=2)
                    for pr in range(B_TILES // 2):
                        bk = bank_f32(next_bank(STAGE_BANKS))
                        planes = bk[:].rearrange("p (u c) -> p u c", u=2)
                        for bl in range(2):
                            words = xm[:, 2 * pr + bl, :].bitcast(F32)
                            for u in range(2):
                                first = 256 * gl + P * u
                                nc.tensor.transpose(
                                    planes[:, u, P * bl : P * (bl + 1)], words[:, first : first + P], ident_f[:]
                                )
                        nc.scalar.copy(
                            out=hw_view[:, 256 * pr : 256 * (pr + 1), :], in_=bk[:].rearrange("p (u c) -> p c u", u=2)
                        )
                drain(1)
                later(lambda: scale_and_quantise_h(c, h_words))

            def quantise_wt(g, grouped):
                nc.vector.quantize_mx(out=wt_codes[:, g, :].bitcast(FP8X4), scales=wt_scales[:, g, :], in_=grouped[:])

            def prepare_w_first(c, share):
                wn = w_in[c]
                for gl in range(CHUNK // K_PASS):
                    g = c * (CHUNK // K_PASS) + gl
                    grouped = stage.tile([P, 4 * D], BF16, name="wtg", tag="wtg", bufs=2, align_bytes=64)
                    g_words = grouped[:].bitcast(F32).rearrange("p (c u) -> p c u", u=2)
                    for j in range(D_TILES // 2):
                        bk = bank_f32(next_bank(STAGE_BANKS))
                        planes = bk[:].rearrange("p (u c) -> p u c", u=2)
                        for dd in range(2):
                            words = wn[:, 2 * j + dd, :].bitcast(F32)
                            for u in range(2):
                                first = 256 * gl + P * u
                                nc.tensor.transpose(
                                    planes[:, u, P * dd : P * (dd + 1)], words[:, first : first + P], ident_f[:]
                                )
                        engine_copy = nc.vector.tensor_copy if (share and j % 2 == 1) else nc.scalar.copy
                        engine_copy(
                            out=g_words[:, 256 * j : 256 * (j + 1), :], in_=bk[:].rearrange("p (u c) -> p c u", u=2)
                        )
                    drain(1)
                    later(lambda g=g, grouped=grouped: quantise_wt(g, grouped))

            load(0)
            load(1)
            mask_x(0)
            counts = bank_f32(COUNT_BANK)
            nc.tensor.matmul(out=counts[:, 0 : 2 * B_TILES], lhsT=ident_b[:], rhs=zeros_b[:], start=True, stop=False)
            for c in range(CHUNKS):
                transpose_x(c)
                prepare_h(c)
                if c + 1 < CHUNKS:
                    mask_x(c + 1)
                prepare_w_first(c, False)
                for nt in range((CHUNK // P) * c, (CHUNK // P) * (c + 1)):
                    count(nt)
                if c + 2 < CHUNKS:
                    load(c + 2)
                elif c + 2 == CHUNKS:
                    reload(0)
                    nc.sync.dma_start(out=gamma_b[:], in_=gamma.partition_broadcast(P))
                    nc.sync.dma_start(out=beta_b[:], in_=beta.partition_broadcast(P))
            nc.tensor.matmul(out=counts[:, 0 : 2 * B_TILES], lhsT=ident_b[:], rhs=zeros_b[:], start=False, stop=True)
            inv_count = const.tile([P, B_TILES], F32, name="inv_count")
            nc.vector.reciprocal(
                out=inv_count[:].rearrange("p (a c) -> p a c", c=1),
                in_=counts[:, 0 : 2 * B_TILES].rearrange("p (a c) -> p a c", c=2)[:, :, 0:1],
            )
            bk = bank_bf16(next_bank(STAGE_BANKS))
            nc.tensor.transpose(bk[:, 0:P], rows_sb[:], ident_b[:])
            nc.vector.tensor_copy(out=bias_cols[:], in_=bk[:, 0 : D_TILES + N_TILES])
            drain(1)
            for j in ORDER[0:2]:
                for gd in range(D_PASSES):
                    regroup_w2(ring_early, stage, "wtg", 2, w_in[CHUNKS - 1], W2_CHUNK * (j % 2), j, gd, V_COLS_TAIL)
                    drain(1)
            drain(0)
            reload(1)

        with tc.tile_pool(name="ring_late", bufs=LATE) as ring_late, tc.tile_pool(name="again", bufs=2) as again, tc.tile_pool(
            name="post", bufs=2
        ) as post, tc.tile_pool(name="small", bufs=2) as small:
            enc_t = post.tile([P, D_TILES, B], F32, name="enc_t", tag="enc_t", bufs=1)
            e_codes = post.tile([P, D_PASSES, B], U32, name="e_codes", tag="e_codes", bufs=1, align_bytes=64)
            e_scales = post.tile([P, D_PASSES, B], U8, name="e_scales", tag="e_scales", bufs=1, align_bytes=64)

            def tanh(acc, d_tile):
                nc.scalar.activation(
                    out=enc_t[:, d_tile, :], in_=acc[:], func=ACT.Tanh, bias=bias_cols[:, d_tile : d_tile + 1]
                )

            def regroup_enc(gd, v_cols):
                grouped = post.tile([P, B, 4], BF16, name="eg", tag="eg", align_bytes=64)
                for engine_copy, lo, hi in ((nc.vector.tensor_copy, 0, v_cols), (nc.scalar.copy, v_cols, B)):
                    if hi > lo:
                        engine_copy(
                            out=grouped[:, lo:hi, :], in_=enc_t[:, 4 * gd : 4 * gd + 4, lo:hi].rearrange("p t b -> p b t")
                        )
                later(
                    lambda: nc.vector.quantize_mx(
                        out=e_codes[:, gd, :].bitcast(FP8X4),
                        scales=e_scales[:, gd, :],
                        in_=grouped[:].rearrange("p b t -> p (b t)"),
                    )
                )

            ln = {}

            def ln_transpose(bt):
                b_cols = slice(P * bt, P * (bt + 1))
                enc = ln_rows[:, bt % 2, :]
                part_sum = small.tile([P, 2], F32, name="part_sum", tag="part_sum")
                for dh in range(2):
                    bk = bank_f32(next_t_bank())
                    for i in range(4):
                        nc.tensor.transpose(bk[:, P * i : P * (i + 1)], enc_t[:, 4 * dh + i, b_cols], ident_f[:])
                    nc.scalar.activation(
                        out=enc[:, BANK_F32 * dh : BANK_F32 * (dh + 1)],
                        in_=bk[:],
                        func=ACT.Copy,
                        accum_out=part_sum[:, dh : dh + 1],
                    )
                ln[bt] = {"enc": enc, "part_sum": part_sum}

            def ln_mean(bt):
                t = ln[bt]
                enc_sum = small.tile([P, 1], F32, name="enc_sum", tag="enc_sum")
                nc.vector.tensor_tensor(out=enc_sum[:], in0=t["part_sum"][:, 0:1], in1=t["part_sum"][:, 1:2], op=ALU.add)
                neg_mean = small.tile([P, 1], F32, name="neg_mean", tag="neg_mean")
                nc.vector.tensor_scalar_mul(out=neg_mean[:], in0=enc_sum[:], scalar1=-1.0 / D)
                t["neg_mean"] = neg_mean

            def ln_square(bt):
                t = ln[bt]
                fin = ln_rows[:, 2 + bt % 2, :]
                sq_sum = small.tile([P, 1], F32, name="sq_sum", tag="sq_sum")
                nc.scalar.activation(out=fin, in_=t["enc"], func=ACT.Square, bias=t["neg_mean"][:], accum_out=sq_sum[:])
                t["fin"] = fin
                t["sq_sum"] = sq_sum

            def ln_rstd(bt):
                t = ln[bt]
                var_eps = small.tile([P, 1], F32, name="var_eps", tag="var_eps")
                nc.vector.tensor_scalar(
                    out=var_eps[:], in0=t["sq_sum"][:], scalar1=1.0 / D, scalar2=LN_EPS, op0=ALU.mult, op1=ALU.add
                )
                rstd = small.tile([P, 1], F32, name="rstd", tag="rstd")
                nc.gpsimd.tensor_tensor(out=rstd[:], in0=var_eps[:], in1=neg_half[:], op=ALU.pow)
                t["rstd"] = rstd

            def ln_final(bt):
                t = ln[bt]
                fin = t["fin"]
                nc.vector.scalar_tensor_tensor(
                    out=fin, in0=t["enc"], scalar=t["neg_mean"][:], in1=gamma_b[:], op0=ALU.add, op1=ALU.mult
                )
                nc.vector.scalar_tensor_tensor(out=fin, in0=fin, scalar=t["rstd"][:], in1=beta_b[:], op0=ALU.mult, op1=ALU.add)
                nc.sync.dma_start(out=out_0[P * bt : P * (bt + 1), :], in_=fin)

            masked = {}

            def difference(j, ntl):
                nt = 4 * j + ntl
                n_cols = slice(P * ntl, P * (ntl + 1))
                acc = bank_f32(next_bank(4))
                for gd in range(D_PASSES):
                    nc.tensor.matmul_mx(
                        out=acc[:],
                        lhsT=w2_codes[j][:, gd, n_cols].bitcast(FP8X4),
                        lhsT_scale=w2_scales[j][:, gd, n_cols],
                        rhs=e_codes[:, gd, :].bitcast(FP8X4),
                        rhs_scale=e_scales[:, gd, :],
                        start=(gd == 0),
                        stop=(gd == D_PASSES - 1),
                    )
                nc.vector.scalar_tensor_tensor(
                    out=masked[j][:, ntl, :],
                    in0=acc[:],
                    scalar=bias_cols[:, D_TILES + nt : D_TILES + nt + 1],
                    in1=nz_t[:, nt, :],
                    op0=ALU.add,
                    op1=ALU.mult,
                )

            def row_sums(j, lo, hi, col):
                for bt in range(B_TILES):
                    bk = bank_f32(next_t_bank())
                    nc.tensor.matmul(
                        out=bk[:, 0 : P * (hi - lo)],
                        lhsT=neg_ident_b[:],
                        rhs=x_nat[:, bt, W2_CHUNK * j + P * lo : W2_CHUNK * j + P * hi],
                        start=True,
                        stop=False,
                    )
                    for ntl in range(lo, hi):
                        nc.tensor.matmul(
                            out=bk[:, P * (ntl - lo) : P * (ntl - lo + 1)],
                            lhsT=masked[j][:, ntl, P * bt : P * (bt + 1)],
                            rhs=ident_f[:],
                            is_transpose=True,
                            start=False,
                            stop=(ntl == hi - 1),
                        )
                    nc.scalar.activation(
                        out=junk[:, 0 : P * (hi - lo)],
                        in_=bk[:, 0 : P * (hi - lo)],
                        func=ACT.Square,
                        accum_out=loss_cols[:, bt, col : col + 1],
                    )

            junk = post.tile([P, BANK_F32], BF16, name="junk", tag="junk", bufs=1)
            loss_cols = post.tile([P, B_TILES, LOSS_COLS], F32, name="loss_cols", tag="loss_cols", bufs=1)

            for d_tile in range(D_TILES):
                j = d_tile // 2
                gd = d_tile % 2
                regroup_w2(ring_late, again, "w2g", 2, w_again[j // 2], W2_CHUNK * (j % 2), j, gd, V_COLS_WINDOW)
                drain(1)
                if d_tile == 3:
                    reload(2)
                acc = bank_f32(d_tile % 4)
                for g in range(N_PASSES):
                    first_matmul(acc, d_tile, g)
                tanh(acc, d_tile)
                if d_tile == 4:
                    regroup_enc(0, B)
                    drain(1)
            drain(0)
            regroup_enc(1, B // 2)
            drain(0)
            m_ring = keep.tile([P, M_SLOTS, 4, B], F32, name="m_ring", tag="wt_codes", align_bytes=64)
            ln_rows = keep.tile([P, 4, D], F32, name="ln_rows", tag="h_codes", align_bytes=64)
            ln_transpose(0)

            last = W2_CHUNKS - 1
            for pos in range(last):
                j = ORDER[pos]
                masked[j] = m_ring[:, pos % M_SLOTS, :, :]
                for ntl in range(4):
                    difference(j, ntl)
                if 1 <= pos <= B_TILES:
                    ln_rstd(pos - 1)
                if pos >= 1:
                    row_sums(ORDER[pos - 1], 0, 4, pos - 1)
                if 1 <= pos <= B_TILES:
                    ln_final(pos - 1)
                if pos < B_TILES:
                    ln_mean(pos)
                    ln_square(pos)
                drain(0)
                if pos + 1 < B_TILES:
                    ln_transpose(pos + 1)
                if EARLY + LATE + pos < W2_CHUNKS:
                    coming = ORDER[EARLY + LATE + pos]
                    for gd in range(D_PASSES):
                        regroup_w2(
                            ring_early, again, "w2g", 2, w_again[coming // 2], W2_CHUNK * (coming % 2), coming, gd, V_COLS_LOOP
                        )

            j = ORDER[last]
            masked[j] = m_ring[:, last % M_SLOTS, :, :]
            difference(j, 0)
            difference(j, 1)
            difference(j, 2)
            difference(j, 3)
            row_sums(ORDER[last - 1], 0, 4, last - 1)
            row_sums(j, 0, 2, last)
            row_sums(j, 2, 4, last + 1)

            totals = small.tile([P, B_TILES], F32, name="totals", tag="totals")
            nc.vector.tensor_reduce(out=totals[:], in_=loss_cols[:], axis=AXIS_X, op=ALU.add)
            per_row = small.tile([P, B_TILES], F32, name="per_row", tag="per_row")
            nc.vector.tensor_tensor(out=per_row[:], in0=totals[:], in1=inv_count[:], op=ALU.mult)
            nc.vector.tensor_reduce(out=spread[:, 0:1], in_=per_row[:], axis=AXIS_X, op=ALU.add)
            bk = bank_f32(next_bank(4))
            nc.tensor.transpose(bk[:, 0:P], spread[:], ident_f[:])
            total = small.tile([P, 1], F32, name="total", tag="total")
            nc.vector.tensor_reduce(out=total[:], in_=bk[:, 0:P], axis=AXIS_X, op=ALU.add)
            nc.sync.dma_start(out=out_1.rearrange("(a b) -> a b", a=1), in_=total[0:1, 0:1])
